import numpy as np
import ml_dtypes


def mxq(x, axis, fmt="e4m3"):
    dtype, down = {"e4m3": (ml_dtypes.float8_e4m3fn, 7), "e5m2": (ml_dtypes.float8_e5m2, 14)}[fmt]
    v = np.moveaxis(np.asarray(x, np.float32).astype(ml_dtypes.bfloat16).astype(np.float64), axis, -1)
    blocks = v.reshape(v.shape[:-1] + (-1, 32))
    amax = np.abs(blocks).max(-1, keepdims=True)
    byte = np.maximum(np.where(amax > 0, np.frexp(amax)[1] - 1 + 127, 0) - down, 1)
    scale = np.exp2(byte - 127.0)
    codes = (blocks / scale).astype(np.float32).astype(dtype).astype(np.float64)
    return np.moveaxis((codes * scale).reshape(v.shape), -1, axis)


WIDE = False


def mx_kscale(k):
    if not WIDE:
        return np.ones(k)
    levels = np.array([10, -10, 5, -5, 0])
    a = np.random.permutation(np.resize(levels, k // 512 * 4)).reshape(k // 512, 4)
    idx = np.arange(k)
    return np.exp2(a[idx // 512, idx % 128 // 32])


BF16 = ml_dtypes.bfloat16


def bf(x):
    return np.asarray(x, np.float32).astype(BF16)


def f64(x):
    return np.asarray(x).astype(np.float64)


B, H, S, T, D = 1, 2, 2048, 512, 1024
DEGREE = 2
EPS = 1e-4


def setup_inputs():
    c = np.exp2(np.round(np.log2(mx_kscale(T)) / 2))
    g = 1.0 / np.sqrt(np.mean(c * c))
    u = np.random.uniform(0.1, 1.5, (B, H, S, 1))
    r = np.where(np.random.random((B, H, S, 1)) < 0.5, np.sqrt(EPS * u / T), 1.0)
    return {"q": bf(np.random.standard_normal((B, H, S, D)) * D ** -0.25 * r * g),
            "k": bf(np.random.standard_normal((B, H, T, D)) * D ** -0.25 * c[:, None]),
            "v": bf(np.random.standard_normal((B, H, T, D)) * 0.3 * np.sqrt(T) / (g * g * c * c)[:, None])}


def reference(q, k, v):
    dots = f64(q) @ f64(k).transpose(0, 1, 3, 2)
    x = dots ** DEGREE
    denom = np.maximum(x.sum(axis=-1, keepdims=True), EPS)
    attn = x / denom
    return mxq(attn, 3, "e4m3") @ mxq(f64(v), 2, "e4m3")

@@ -1,0 +1,250 @@
+from contextlib import ExitStack
+
+import concourse.masks as masks
+import concourse.mybir as mybir
+
+BF16 = mybir.dt.bfloat16
+F32 = mybir.dt.float32
+U32 = mybir.dt.uint32
+U8 = mybir.dt.uint8
+FP8X4 = mybir.dt.float8_e4m3fn_x4
+SQUARE = mybir.ActivationFunctionType.Square
+
+P = 128
+HEADS, S, T, D = 2, 2048, 512, 1024
+EPS = 1e-4
+PACK = 4
+PAIR = 2
+CHUNKS = D // P
+BANK = 512
+HALVES = D // BANK
+ROUNDS_PER_HEAD = S // (PAIR * P)
+ROUNDS = HEADS * ROUNDS_PER_HEAD
+FLIPS_PER_MATMUL = 2
+DRAIN_STEPS = 3
+
+FLOPS = 2 * 2 * HEADS * S * T * D
+
+assert T == PACK * P
+assert 2 * CHUNKS <= CHUNKS * FLIPS_PER_MATMUL
+
+
+def tile_polynomialattn_t_kernel(tc, q, k, v, out):
+    nc = tc.nc
+
+    q_rounds = q.rearrange("b h (r p u) d -> (b h r) p u d", p=P, u=PAIR)
+    out_rounds = out.rearrange("b h (r p u) d -> (b h r) p u d", p=P, u=PAIR)
+    k_pieces = k.rearrange("b h (p j) d -> (b h) j p d", j=PACK)
+    v_heads = v.rearrange("b h (p j) d -> (b h) p j d", j=PACK)
+
+    with ExitStack() as ctx:
+        keep = ctx.enter_context(tc.tile_pool(name="keep", bufs=1))
+        hand = ctx.enter_context(tc.tile_pool(name="hand", bufs=2))
+        turned = ctx.enter_context(tc.tile_pool(name="turned", bufs=2 * PAIR))
+        leaving = ctx.enter_context(tc.tile_pool(name="leaving", bufs=3 * PAIR))
+        dots_banks = ctx.enter_context(tc.psum_pool(name="dots_banks", bufs=PAIR))
+        flip_banks = ctx.enter_context(tc.psum_pool(name="flip_banks", bufs=2))
+        prod_banks = ctx.enter_context(tc.psum_pool(name="prod_banks", bufs=PAIR * HALVES))
+        ctx.enter_context(tc.manual_schedule())
+
+        identity = keep.tile([P, P], BF16, name="identity")
+        masks.make_identity(nc, identity[:])
+
+        q_raw, k_raw, v_raw = {}, {}, {}
+
+        def load_q(i):
+            q_raw[i] = keep.tile([P, PAIR, D], BF16, name="q_raw%d" % i)
+            nc.sync.dma_start(out=q_raw[i][:], in_=q_rounds[i])
+
+        def load_k(h):
+            for j in range(PACK):
+                k_raw[(h, j)] = keep.tile([P, D], BF16, name="k_raw%d_%d" % (h, j))
+                nc.sync.dma_start(out=k_raw[(h, j)][:], in_=k_pieces[h, j])
+
+        def load_v(h):
+            v_raw[h] = keep.tile([P, PACK, D], BF16, name="v_raw%d" % h)
+            nc.sync.dma_start(out=v_raw[h][:], in_=v_heads[h])
+
+        load_k(0)
+        load_q(0)
+        load_q(1)
+        load_v(0)
+        load_q(2)
+        load_v(1)
+        load_q(3)
+        load_k(1)
+        for i in range(4, ROUNDS):
+            load_q(i)
+
+        k_turned, v_codes, v_scales = {}, {}, {}
+        for h in range(HEADS):
+            k_turned[h] = keep.tile([P, CHUNKS, T], BF16, name="k_turned%d" % h)
+            v_codes[h] = keep.tile([P, D], U32, name="v_codes%d" % h, align_bytes=64)
+            v_scales[h] = keep.tile([P, D], U8, name="v_scales%d" % h, align_bytes=64)
+
+        q_turned, x, row_sums, attn, attn_grouped, attn_codes, attn_scales = {}, {}, {}, {}, {}, {}, {}
+        v_grouped, products = {}, {}
+
+        def is_round(i):
+            return 0 <= i < ROUNDS
+
+        def flips_into(bank, blocks):
+            return [(bank[:, n, :], block) for n, block in enumerate(blocks)]
+
+        def new_flip_bank():
+            bank = flip_banks.tile([P, CHUNKS, P], BF16, name="flip_bank")
+            return bank
+
+        def multiply_qk(i, u, flips):
+            dots = None
+            if is_round(i):
+                dots = dots_banks.tile([P, T], F32, name="dots")
+            for c in range(CHUNKS):
+                if is_round(i):
+                    nc.tensor.matmul(
+                        out=dots[:],
+                        lhsT=q_turned[(i, u)][:, c, :],
+                        rhs=k_turned[i // ROUNDS_PER_HEAD][:, c, :],
+                        start=(c == 0),
+                        stop=(c == CHUNKS - 1),
+                    )
+                for target, block in flips[c * FLIPS_PER_MATMUL : (c + 1) * FLIPS_PER_MATMUL]:
+                    nc.tensor.transpose(target, block, identity[:])
+            return dots
+
+        def square(i, u, dots):
+            if not is_round(i):
+                return
+            if u == 0:
+                x[i] = hand.tile([P, PAIR, T], F32, name="x")
+                row_sums[i] = hand.tile([P, PAIR], F32, name="row_sums")
+            nc.scalar.activation(
+                out=x[i][:, u, :], in_=dots[:], func=SQUARE, accum_out=row_sums[i][:, u : u + 1]
+            )
+
+        def normalise(i):
+            if not is_round(i):
+                return
+            denom = hand.tile([P, PAIR], F32, name="denom")
+            nc.vector.tensor_scalar_max(out=denom[:], in0=row_sums[i][:], scalar1=EPS)
+            inverse = hand.tile([P, PAIR], F32, name="inverse")
+            nc.vector.reciprocal(out=inverse[:], in_=denom[:])
+            attn[i] = hand.tile([P, PAIR, T], BF16, name="attn")
+            for u in range(PAIR):
+                nc.vector.tensor_scalar_mul(
+                    out=attn[i][:, u, :], in0=x[i][:, u, :], scalar1=inverse[:, u : u + 1]
+                )
+
+        def regroup_attn(i, bank):
+            attn_grouped[i] = hand.tile([P, PAIR, P, PACK], BF16, name="attn_grouped", align_bytes=64)
+            nc.vector.tensor_copy(
+                out=attn_grouped[i][:], in_=bank[:].rearrange("p (u j) s -> p u s j", u=PAIR)
+            )
+
+        def quantise_attn(i):
+            if not is_round(i):
+                return
+            attn_codes[i] = hand.tile([P, PAIR * P], U32, name="attn_codes", align_bytes=64)
+            attn_scales[i] = hand.tile([P, PAIR * P], U8, name="attn_scales", align_bytes=64)
+            nc.vector.quantize_mx(
+                out=attn_codes[i][:].bitcast(FP8X4),
+                scales=attn_scales[i][:],
+                in_=attn_grouped[i][:].rearrange("p u s j -> p (u s j)"),
+            )
+
+        def regroup_v(n):
+            if not 0 <= n < HEADS * HALVES:
+                return
+            cols = slice((n % HALVES) * BANK, (n % HALVES + 1) * BANK)
+            v_grouped[n] = hand.tile([P, BANK, PACK], BF16, name="v_grouped", align_bytes=64)
+            nc.vector.tensor_copy(
+                out=v_grouped[n][:], in_=v_raw[n // HALVES][:, :, cols].rearrange("p j d -> p d j")
+            )
+
+        def quantise_v(n):
+            if not 0 <= n < HEADS * HALVES:
+                return
+            cols = slice((n % HALVES) * BANK, (n % HALVES + 1) * BANK)
+            nc.vector.quantize_mx(
+                out=v_codes[n // HALVES][:, cols].bitcast(FP8X4),
+                scales=v_scales[n // HALVES][:, cols],
+                in_=v_grouped[n][:].rearrange("p d j -> p (d j)"),
+            )
+
+        def multiply_mx(i):
+            if not is_round(i):
+                return
+            h = i // ROUNDS_PER_HEAD
+            for u in range(PAIR):
+                queries = slice(u * P, (u + 1) * P)
+                for half in range(HALVES):
+                    cols = slice(half * BANK, (half + 1) * BANK)
+                    products[(i, u, half)] = prod_banks.tile([P, BANK], F32, name="product")
+                    nc.tensor.matmul_mx(
+                        out=products[(i, u, half)][:],
+                        lhsT=attn_codes[i][:, queries].bitcast(FP8X4),
+                        lhsT_scale=attn_scales[i][:, queries],
+                        rhs=v_codes[h][:, cols].bitcast(FP8X4),
+                        rhs_scale=v_scales[h][:, cols],
+                        start=True,
+                        stop=True,
+                    )
+
+        def store_products(i):
+            if not is_round(i):
+                return
+            for u in range(PAIR):
+                result = leaving.tile([P, D], F32, name="result")
+                for half in range(HALVES):
+                    cols = slice(half * BANK, (half + 1) * BANK)
+                    if u == 0:
+                        nc.scalar.copy(out=result[:, cols], in_=products[(i, u, half)][:])
+                    else:
+                        nc.vector.tensor_copy(out=result[:, cols], in_=products[(i, u, half)][:])
+                nc.sync.dma_start(out=out_rounds[i][:, u, :], in_=result[:])
+
+        for i in range(-PACK, ROUNDS + DRAIN_STEPS):
+            normalise(i - 1)
+            quantise_attn(i - 2)
+            quantise_v(i - 1)
+            store_products(i - 3)
+
+            q_flips, q_banks = [], []
+            if is_round(i + 1):
+                for u in range(PAIR):
+                    q_banks.append(new_flip_bank())
+                    q_flips.extend(
+                        flips_into(q_banks[u], [q_raw[i + 1][:, u, c * P : (c + 1) * P] for c in range(CHUNKS)])
+                    )
+            dots = multiply_qk(i, 0, q_flips)
+            for u, bank in enumerate(q_banks):
+                q_turned[(i + 1, u)] = turned.tile([P, CHUNKS, P], BF16, name="q_turned")
+                nc.scalar.copy(out=q_turned[(i + 1, u)][:], in_=bank[:])
+            square(i, 0, dots)
+            regroup_v(i)
+
+            late_flips = []
+            attn_bank, k_bank = None, None
+            if is_round(i - 1):
+                attn_bank = new_flip_bank()
+                late_flips.extend(
+                    flips_into(
+                        attn_bank,
+                        [attn[i - 1][:, u, j * P : (j + 1) * P] for u in range(PAIR) for j in range(PACK)],
+                    )
+                )
+            next_head = i // ROUNDS_PER_HEAD + 1
+            piece = i % ROUNDS_PER_HEAD - (ROUNDS_PER_HEAD - PACK)
+            if next_head < HEADS and piece >= 0:
+                k_bank = new_flip_bank()
+                late_flips.extend(
+                    flips_into(k_bank, [k_raw[(next_head, piece)][:, c * P : (c + 1) * P] for c in range(CHUNKS)])
+                )
+            dots = multiply_qk(i, 1, late_flips)
+            if attn_bank is not None:
+                regroup_attn(i - 1, attn_bank)
+            square(i, 1, dots)
+            if k_bank is not None:
+                nc.scalar.copy(out=k_turned[next_head][:, :, piece * P : (piece + 1) * P], in_=k_bank[:])
+
+            multiply_mx(i - 2)

@@ -18,33 +18,38 @@ PAIR = 2
 CHUNKS = D // P
 BANK = 512
 HALVES = D // BANK
-ROUNDS_PER_HEAD = S // (PAIR * P)
-ROUNDS = HEADS * ROUNDS_PER_HEAD
-FLIPS_PER_MATMUL = 2
-DRAIN_STEPS = 3
+TILES_PER_HEAD = S // P
+TILES = HEADS * TILES_PER_HEAD
+
+Q_LEAD = 2
+FLIP_LAG = 2
+QUANT_LAG = 3
+MX_LAG = 5
+OUT_LAG = 6
+K_STRIDE = 2
+FLIPS_PER_MATMUL = 3
 
 FLOPS = 2 * 2 * HEADS * S * T * D
 
 assert T == PACK * P
-assert 2 * CHUNKS <= CHUNKS * FLIPS_PER_MATMUL
+assert PACK + 2 * CHUNKS <= (CHUNKS - 1) * FLIPS_PER_MATMUL
 
 
 def tile_polynomialattn_t_kernel(tc, q, k, v, out):
     nc = tc.nc
 
-    q_rounds = q.rearrange("b h (r p u) d -> (b h r) p u d", p=P, u=PAIR)
-    out_rounds = out.rearrange("b h (r p u) d -> (b h r) p u d", p=P, u=PAIR)
+    q_pairs = q.rearrange("b h (r p u) d -> (b h r) p u d", p=P, u=PAIR)
+    out_pairs = out.rearrange("b h (r p u) d -> (b h r) p u d", p=P, u=PAIR)
     k_pieces = k.rearrange("b h (p j) d -> (b h) j p d", j=PACK)
     v_heads = v.rearrange("b h (p j) d -> (b h) p j d", j=PACK)
 
     with ExitStack() as ctx:
         keep = ctx.enter_context(tc.tile_pool(name="keep", bufs=1))
-        hand = ctx.enter_context(tc.tile_pool(name="hand", bufs=2))
-        turned = ctx.enter_context(tc.tile_pool(name="turned", bufs=2 * PAIR))
-        leaving = ctx.enter_context(tc.tile_pool(name="leaving", bufs=3 * PAIR))
-        dots_banks = ctx.enter_context(tc.psum_pool(name="dots_banks", bufs=PAIR))
-        flip_banks = ctx.enter_context(tc.psum_pool(name="flip_banks", bufs=2))
-        prod_banks = ctx.enter_context(tc.psum_pool(name="prod_banks", bufs=PAIR * HALVES))
+        hand = ctx.enter_context(tc.tile_pool(name="hand", bufs=MX_LAG - QUANT_LAG + 2))
+        v_stage = ctx.enter_context(tc.tile_pool(name="v_stage", bufs=2))
+        dots_banks = ctx.enter_context(tc.psum_pool(name="dots_banks", bufs=2))
+        flip_banks = ctx.enter_context(tc.psum_pool(name="flip_banks", bufs=4))
+        prod_banks = ctx.enter_context(tc.psum_pool(name="prod_banks", bufs=HALVES))
         ctx.enter_context(tc.manual_schedule())
 
         identity = keep.tile([P, P], BF16, name="identity")
@@ -52,9 +57,9 @@ def tile_polynomialattn_t_kernel(tc, q, k, v, out):
 
         q_raw, k_raw, v_raw = {}, {}, {}
 
-        def load_q(i):
-            q_raw[i] = keep.tile([P, PAIR, D], BF16, name="q_raw%d" % i)
-            nc.sync.dma_start(out=q_raw[i][:], in_=q_rounds[i])
+        def load_q(r):
+            q_raw[r] = keep.tile([P, PAIR, D], BF16, name="q_raw%d" % r)
+            nc.sync.dma_start(out=q_raw[r][:], in_=q_pairs[r])
 
         def load_k(h):
             for j in range(PACK):
@@ -73,8 +78,8 @@ def tile_polynomialattn_t_kernel(tc, q, k, v, out):
         load_v(1)
         load_q(3)
         load_k(1)
-        for i in range(4, ROUNDS):
-            load_q(i)
+        for r in range(4, TILES // PAIR):
+            load_q(r)
 
         k_turned, v_codes, v_scales = {}, {}, {}
         for h in range(HEADS):
@@ -82,29 +87,32 @@ def tile_polynomialattn_t_kernel(tc, q, k, v, out):
             v_codes[h] = keep.tile([P, D], U32, name="v_codes%d" % h, align_bytes=64)
             v_scales[h] = keep.tile([P, D], U8, name="v_scales%d" % h, align_bytes=64)
 
-        q_turned, x, row_sums, attn, attn_grouped, attn_codes, attn_scales = {}, {}, {}, {}, {}, {}, {}
+        q_turned, x, row_sum, attn, attn_grouped, attn_codes, attn_scales = {}, {}, {}, {}, {}, {}, {}
         v_grouped, products = {}, {}
 
-        def is_round(i):
-            return 0 <= i < ROUNDS
+        def is_tile(m):
+            return 0 <= m < TILES
 
-        def flips_into(bank, blocks):
-            return [(bank[:, n, :], block) for n, block in enumerate(blocks)]
+        def is_v_half(n):
+            return 0 <= n < HEADS * HALVES
 
         def new_flip_bank():
             bank = flip_banks.tile([P, CHUNKS, P], BF16, name="flip_bank")
             return bank
 
-        def multiply_qk(i, u, flips):
+        def flips_into(bank, blocks):
+            return [(bank[:, n, :], block) for n, block in enumerate(blocks)]
+
+        def multiply_qk(m, flips):
             dots = None
-            if is_round(i):
+            if is_tile(m):
                 dots = dots_banks.tile([P, T], F32, name="dots")
             for c in range(CHUNKS):
-                if is_round(i):
+                if is_tile(m):
                     nc.tensor.matmul(
                         out=dots[:],
-                        lhsT=q_turned[(i, u)][:, c, :],
-                        rhs=k_turned[i // ROUNDS_PER_HEAD][:, c, :],
+                        lhsT=q_turned[m][:, c, :],
+                        rhs=k_turned[m // TILES_PER_HEAD][:, c, :],
                         start=(c == 0),
                         stop=(c == CHUNKS - 1),
                     )
@@ -112,57 +120,49 @@ def tile_polynomialattn_t_kernel(tc, q, k, v, out):
                     nc.tensor.transpose(target, block, identity[:])
             return dots
 
-        def square(i, u, dots):
-            if not is_round(i):
+        def square(m, dots):
+            if not is_tile(m):
                 return
-            if u == 0:
-                x[i] = hand.tile([P, PAIR, T], F32, name="x")
-                row_sums[i] = hand.tile([P, PAIR], F32, name="row_sums")
-            nc.scalar.activation(
-                out=x[i][:, u, :], in_=dots[:], func=SQUARE, accum_out=row_sums[i][:, u : u + 1]
-            )
+            x[m] = hand.tile([P, T], F32, name="x")
+            row_sum[m] = hand.tile([P, 1], F32, name="row_sum")
+            nc.scalar.activation(out=x[m][:], in_=dots[:], func=SQUARE, accum_out=row_sum[m][:])
 
-        def normalise(i):
-            if not is_round(i):
+        def normalise(m):
+            if not is_tile(m):
                 return
-            denom = hand.tile([P, PAIR], F32, name="denom")
-            nc.vector.tensor_scalar_max(out=denom[:], in0=row_sums[i][:], scalar1=EPS)
-            inverse = hand.tile([P, PAIR], F32, name="inverse")
+            denom = hand.tile([P, 1], F32, name="denom")
+            nc.vector.tensor_scalar_max(out=denom[:], in0=row_sum[m][:], scalar1=EPS)
+            inverse = hand.tile([P, 1], F32, name="inverse")
             nc.vector.reciprocal(out=inverse[:], in_=denom[:])
-            attn[i] = hand.tile([P, PAIR, T], BF16, name="attn")
-            for u in range(PAIR):
-                nc.vector.tensor_scalar_mul(
-                    out=attn[i][:, u, :], in0=x[i][:, u, :], scalar1=inverse[:, u : u + 1]
-                )
+            attn[m] = hand.tile([P, T], BF16, name="attn")
+            nc.vector.tensor_scalar_mul(out=attn[m][:], in0=x[m][:], scalar1=inverse[:])
 
-        def regroup_attn(i, bank):
-            attn_grouped[i] = hand.tile([P, PAIR, P, PACK], BF16, name="attn_grouped", align_bytes=64)
-            nc.vector.tensor_copy(
-                out=attn_grouped[i][:], in_=bank[:].rearrange("p (u j) s -> p u s j", u=PAIR)
-            )
+        def regroup_attn(m, bank):
+            attn_grouped[m] = hand.tile([P, P, PACK], BF16, name="attn_grouped", align_bytes=64)
+            nc.vector.tensor_copy(out=attn_grouped[m][:], in_=bank[:, :PACK, :].rearrange("p j s -> p s j"))
 
-        def quantise_attn(i):
-            if not is_round(i):
+        def quantise_attn(m):
+            if not is_tile(m):
                 return
-            attn_codes[i] = hand.tile([P, PAIR * P], U32, name="attn_codes", align_bytes=64)
-            attn_scales[i] = hand.tile([P, PAIR * P], U8, name="attn_scales", align_bytes=64)
+            attn_codes[m] = hand.tile([P, P], U32, name="attn_codes", align_bytes=64)
+            attn_scales[m] = hand.tile([P, P], U8, name="attn_scales", align_bytes=64)
             nc.vector.quantize_mx(
-                out=attn_codes[i][:].bitcast(FP8X4),
-                scales=attn_scales[i][:],
-                in_=attn_grouped[i][:].rearrange("p u s j -> p (u s j)"),
+                out=attn_codes[m][:].bitcast(FP8X4),
+                scales=attn_scales[m][:],
+                in_=attn_grouped[m][:].rearrange("p s j -> p (s j)"),
             )
 
         def regroup_v(n):
-            if not 0 <= n < HEADS * HALVES:
+            if not is_v_half(n):
                 return
             cols = slice((n % HALVES) * BANK, (n % HALVES + 1) * BANK)
-            v_grouped[n] = hand.tile([P, BANK, PACK], BF16, name="v_grouped", align_bytes=64)
+            v_grouped[n] = v_stage.tile([P, BANK, PACK], BF16, name="v_grouped", align_bytes=64)
             nc.vector.tensor_copy(
                 out=v_grouped[n][:], in_=v_raw[n // HALVES][:, :, cols].rearrange("p j d -> p d j")
             )
 
         def quantise_v(n):
-            if not 0 <= n < HEADS * HALVES:
+            if not is_v_half(n):
                 return
             cols = slice((n % HALVES) * BANK, (n % HALVES + 1) * BANK)
             nc.vector.quantize_mx(
@@ -171,80 +171,66 @@ def tile_polynomialattn_t_kernel(tc, q, k, v, out):
                 in_=v_grouped[n][:].rearrange("p d j -> p (d j)"),
             )
 
-        def multiply_mx(i):
-            if not is_round(i):
+        def multiply_mx(m):
+            if not is_tile(m):
                 return
-            h = i // ROUNDS_PER_HEAD
-            for u in range(PAIR):
-                queries = slice(u * P, (u + 1) * P)
-                for half in range(HALVES):
-                    cols = slice(half * BANK, (half + 1) * BANK)
-                    products[(i, u, half)] = prod_banks.tile([P, BANK], F32, name="product")
-                    nc.tensor.matmul_mx(
-                        out=products[(i, u, half)][:],
-                        lhsT=attn_codes[i][:, queries].bitcast(FP8X4),
-                        lhsT_scale=attn_scales[i][:, queries],
-                        rhs=v_codes[h][:, cols].bitcast(FP8X4),
-                        rhs_scale=v_scales[h][:, cols],
-                        start=True,
-                        stop=True,
-                    )
+            h = m // TILES_PER_HEAD
+            for half in range(HALVES):
+                cols = slice(half * BANK, (half + 1) * BANK)
+                products[(m, half)] = prod_banks.tile([P, BANK], F32, name="product")
+                nc.tensor.matmul_mx(
+                    out=products[(m, half)][:],
+                    lhsT=attn_codes[m][:].bitcast(FP8X4),
+                    lhsT_scale=attn_scales[m][:],
+                    rhs=v_codes[h][:, cols].bitcast(FP8X4),
+                    rhs_scale=v_scales[h][:, cols],
+                    start=True,
+                    stop=True,
+                )
 
-        def store_products(i):
-            if not is_round(i):
+        def store_products(m):
+            if not is_tile(m):
                 return
-            for u in range(PAIR):
-                result = leaving.tile([P, D], F32, name="result")
-                for half in range(HALVES):
-                    cols = slice(half * BANK, (half + 1) * BANK)
-                    if u == 0:
-                        nc.scalar.copy(out=result[:, cols], in_=products[(i, u, half)][:])
-                    else:
-                        nc.vector.tensor_copy(out=result[:, cols], in_=products[(i, u, half)][:])
-                nc.sync.dma_start(out=out_rounds[i][:, u, :], in_=result[:])
+            result = hand.tile([P, D], F32, name="result")
+            nc.scalar.copy(out=result[:, :BANK], in_=products[(m, 0)][:])
+            nc.vector.tensor_copy(out=result[:, BANK:], in_=products[(m, 1)][:])
+            nc.sync.dma_start(out=out_pairs[m // PAIR][:, m % PAIR, :], in_=result[:])
 
-        for i in range(-PACK, ROUNDS + DRAIN_STEPS):
-            normalise(i - 1)
-            quantise_attn(i - 2)
-            quantise_v(i - 1)
-            store_products(i - 3)
+        for m in range(-K_STRIDE * PACK, TILES + OUT_LAG):
+            store_products(m - OUT_LAG)
+            normalise(m - 1)
+            quantise_attn(m - QUANT_LAG)
+            quantise_v(m - 1)
 
-            q_flips, q_banks = [], []
-            if is_round(i + 1):
-                for u in range(PAIR):
-                    q_banks.append(new_flip_bank())
-                    q_flips.extend(
-                        flips_into(q_banks[u], [q_raw[i + 1][:, u, c * P : (c + 1) * P] for c in range(CHUNKS)])
-                    )
-            dots = multiply_qk(i, 0, q_flips)
-            for u, bank in enumerate(q_banks):
-                q_turned[(i + 1, u)] = turned.tile([P, CHUNKS, P], BF16, name="q_turned")
-                nc.scalar.copy(out=q_turned[(i + 1, u)][:], in_=bank[:])
-            square(i, 0, dots)
-            regroup_v(i)
-
-            late_flips = []
-            attn_bank, k_bank = None, None
-            if is_round(i - 1):
+            flips = []
+            attn_bank, q_bank, k_bank = None, None, None
+            if is_tile(m - FLIP_LAG):
                 attn_bank = new_flip_bank()
-                late_flips.extend(
-                    flips_into(
-                        attn_bank,
-                        [attn[i - 1][:, u, j * P : (j + 1) * P] for u in range(PAIR) for j in range(PACK)],
-                    )
+                flips.extend(
+                    flips_into(attn_bank, [attn[m - FLIP_LAG][:, j * P : (j + 1) * P] for j in range(PACK)])
                 )
-            next_head = i // ROUNDS_PER_HEAD + 1
-            piece = i % ROUNDS_PER_HEAD - (ROUNDS_PER_HEAD - PACK)
-            if next_head < HEADS and piece >= 0:
+            if is_tile(m + Q_LEAD):
+                q_bank = new_flip_bank()
+                q_tile = q_raw[(m + Q_LEAD) // PAIR][:, (m + Q_LEAD) % PAIR, :]
+                flips.extend(flips_into(q_bank, [q_tile[:, c * P : (c + 1) * P] for c in range(CHUNKS)]))
+            head, steps_in = divmod(m + K_STRIDE * PACK, TILES_PER_HEAD)
+            piece = steps_in // K_STRIDE
+            if head < HEADS and piece < PACK and steps_in % K_STRIDE == 0:
                 k_bank = new_flip_bank()
-                late_flips.extend(
-                    flips_into(k_bank, [k_raw[(next_head, piece)][:, c * P : (c + 1) * P] for c in range(CHUNKS)])
+                flips.extend(
+                    flips_into(k_bank, [k_raw[(head, piece)][:, c * P : (c + 1) * P] for c in range(CHUNKS)])
                 )
-            dots = multiply_qk(i, 1, late_flips)
-            if attn_bank is not None:
-                regroup_attn(i - 1, attn_bank)
-            square(i, 1, dots)
-            if k_bank is not None:
-                nc.scalar.copy(out=k_turned[next_head][:, :, piece * P : (piece + 1) * P], in_=k_bank[:])
 
-            multiply_mx(i - 2)
+            dots = multiply_qk(m, flips)
+
+            if attn_bank is not None:
+                regroup_attn(m - FLIP_LAG, attn_bank)
+            if q_bank is not None:
+                q_turned[m + Q_LEAD] = hand.tile([P, CHUNKS, P], BF16, name="q_turned")
+                nc.scalar.copy(out=q_turned[m + Q_LEAD][:], in_=q_bank[:])
+            if k_bank is not None:
+                nc.scalar.copy(out=k_turned[head][:, :, piece * P : (piece + 1) * P], in_=k_bank[:])
+            regroup_v(m)
+            square(m, dots)
+
+            multiply_mx(m - MX_LAG)

@@ -15,24 +15,26 @@ HEADS, S, T, D = 2, 2048, 512, 1024
 EPS = 1e-4
 PACK = 4
 PAIR = 2
-CHUNKS = D // P
+GROUPS = D // (PAIR * P)
 BANK = 512
 HALVES = D // BANK
 TILES_PER_HEAD = S // P
 TILES = HEADS * TILES_PER_HEAD
+MATMULS = GROUPS * PAIR
 
 Q_LEAD = 2
-FLIP_LAG = 2
-QUANT_LAG = 3
-MX_LAG = 5
+FLIP_LAG = 3
+QUANT_LAG = 4
+MX_LAG = 4
 OUT_LAG = 6
 K_STRIDE = 2
-FLIPS_PER_MATMUL = 3
+FLIPS_PER_MATMUL = 2
+ATTN_FIRST, Q_FIRST, K_FIRST = 0, 2, 6
+WARM_MATMULS = 16
 
 FLOPS = 2 * 2 * HEADS * S * T * D
 
-assert T == PACK * P
-assert PACK + 2 * CHUNKS <= (CHUNKS - 1) * FLIPS_PER_MATMUL
+assert T == PACK * P and K_STRIDE % 2 == 0 and MX_LAG % 2 == 0
 
 
 def tile_polynomialattn_t_kernel(tc, q, k, v, out):
@@ -45,15 +47,21 @@ def tile_polynomialattn_t_kernel(tc, q, k, v, out):
 
     with ExitStack() as ctx:
         keep = ctx.enter_context(tc.tile_pool(name="keep", bufs=1))
-        hand = ctx.enter_context(tc.tile_pool(name="hand", bufs=MX_LAG - QUANT_LAG + 2))
+        hand = ctx.enter_context(tc.tile_pool(name="hand", bufs=4))
         v_stage = ctx.enter_context(tc.tile_pool(name="v_stage", bufs=2))
         dots_banks = ctx.enter_context(tc.psum_pool(name="dots_banks", bufs=2))
-        flip_banks = ctx.enter_context(tc.psum_pool(name="flip_banks", bufs=4))
-        prod_banks = ctx.enter_context(tc.psum_pool(name="prod_banks", bufs=HALVES))
+        flip_banks = ctx.enter_context(tc.psum_pool(name="flip_banks", bufs=2))
+        prod_banks = ctx.enter_context(tc.psum_pool(name="prod_banks", bufs=PAIR * HALVES))
         ctx.enter_context(tc.manual_schedule())
 
         identity = keep.tile([P, P], BF16, name="identity")
         masks.make_identity(nc, identity[:])
+        identity_words = keep.tile([P, P], F32, name="identity_words")
+        masks.make_identity(nc, identity_words[:])
+
+        warm = dots_banks.tile([P, T], F32, name="dots")
+        for n in range(WARM_MATMULS):
+            nc.tensor.matmul(out=warm[:, :P], lhsT=identity[:], rhs=identity[:], start=True, stop=True)
 
         q_raw, k_raw, v_raw = {}, {}, {}
 
@@ -61,29 +69,31 @@ def tile_polynomialattn_t_kernel(tc, q, k, v, out):
             q_raw[r] = keep.tile([P, PAIR, D], BF16, name="q_raw%d" % r)
             nc.sync.dma_start(out=q_raw[r][:], in_=q_pairs[r])
 
-        def load_k(h):
-            for j in range(PACK):
-                k_raw[(h, j)] = keep.tile([P, D], BF16, name="k_raw%d_%d" % (h, j))
-                nc.sync.dma_start(out=k_raw[(h, j)][:], in_=k_pieces[h, j])
+        def load_k(h, j):
+            k_raw[(h, j)] = keep.tile([P, D], BF16, name="k_raw%d_%d" % (h, j))
+            nc.sync.dma_start(out=k_raw[(h, j)][:], in_=k_pieces[h, j])
 
         def load_v(h):
             v_raw[h] = keep.tile([P, PACK, D], BF16, name="v_raw%d" % h)
             nc.sync.dma_start(out=v_raw[h][:], in_=v_heads[h])
 
-        load_k(0)
+        for j in range(PACK - 1):
+            load_k(0, j)
         load_q(0)
+        load_k(0, PACK - 1)
         load_q(1)
         load_v(0)
         load_q(2)
         load_v(1)
         load_q(3)
-        load_k(1)
+        for j in range(PACK):
+            load_k(1, j)
         for r in range(4, TILES // PAIR):
             load_q(r)
 
         k_turned, v_codes, v_scales = {}, {}, {}
         for h in range(HEADS):
-            k_turned[h] = keep.tile([P, CHUNKS, T], BF16, name="k_turned%d" % h)
+            k_turned[h] = keep.tile([P, GROUPS, PAIR * T], BF16, name="k_turned%d" % h)
             v_codes[h] = keep.tile([P, D], U32, name="v_codes%d" % h, align_bytes=64)
             v_scales[h] = keep.tile([P, D], U8, name="v_scales%d" % h, align_bytes=64)
 
@@ -96,28 +106,33 @@ def tile_polynomialattn_t_kernel(tc, q, k, v, out):
         def is_v_half(n):
             return 0 <= n < HEADS * HALVES
 
-        def new_flip_bank():
-            bank = flip_banks.tile([P, CHUNKS, P], BF16, name="flip_bank")
-            return bank
+        def word_flips(bank, row_tile):
+            words = row_tile.bitcast(F32)
+            return [(bank[:, g, :], words[:, g * P : (g + 1) * P], identity_words) for g in range(GROUPS)]
 
-        def flips_into(bank, blocks):
-            return [(bank[:, n, :], block) for n, block in enumerate(blocks)]
+        def attn_flips(bank, m):
+            return [(bank[:, j, :], attn[m][:, j * P : (j + 1) * P], identity) for j in range(PACK)]
 
-        def multiply_qk(m, flips):
+        def weave(behind, first, flips):
+            for n, flip in enumerate(flips):
+                behind[first + n // FLIPS_PER_MATMUL].append(flip)
+
+        def multiply_qk(m, behind):
             dots = None
             if is_tile(m):
                 dots = dots_banks.tile([P, T], F32, name="dots")
-            for c in range(CHUNKS):
+            for n in range(MATMULS):
+                g, e = divmod(n, PAIR)
                 if is_tile(m):
                     nc.tensor.matmul(
                         out=dots[:],
-                        lhsT=q_turned[m][:, c, :],
-                        rhs=k_turned[m // TILES_PER_HEAD][:, c, :],
-                        start=(c == 0),
-                        stop=(c == CHUNKS - 1),
+                        lhsT=q_turned[m][:, g, e : PAIR * P : PAIR],
+                        rhs=k_turned[m // TILES_PER_HEAD][:, g, e : PAIR * T : PAIR],
+                        start=(n == 0),
+                        stop=(n == MATMULS - 1),
                     )
-                for target, block in flips[c * FLIPS_PER_MATMUL : (c + 1) * FLIPS_PER_MATMUL]:
-                    nc.tensor.transpose(target, block, identity[:])
+                for target, block, one in behind[n]:
+                    nc.tensor.transpose(target, block, one[:])
             return dots
 
         def square(m, dots):
@@ -139,7 +154,7 @@ def tile_polynomialattn_t_kernel(tc, q, k, v, out):
 
         def regroup_attn(m, bank):
             attn_grouped[m] = hand.tile([P, P, PACK], BF16, name="attn_grouped", align_bytes=64)
-            nc.vector.tensor_copy(out=attn_grouped[m][:], in_=bank[:, :PACK, :].rearrange("p j s -> p s j"))
+            nc.vector.tensor_copy(out=attn_grouped[m][:], in_=bank[:].rearrange("p j s -> p s j"))
 
         def quantise_attn(m):
             if not is_tile(m):
@@ -197,40 +212,39 @@ def tile_polynomialattn_t_kernel(tc, q, k, v, out):
             nc.sync.dma_start(out=out_pairs[m // PAIR][:, m % PAIR, :], in_=result[:])
 
         for m in range(-K_STRIDE * PACK, TILES + OUT_LAG):
-            store_products(m - OUT_LAG)
-            normalise(m - 1)
             quantise_attn(m - QUANT_LAG)
-            quantise_v(m - 1)
+            store_products(m - OUT_LAG)
 
-            flips = []
+            behind = [[] for n in range(MATMULS)]
             attn_bank, q_bank, k_bank = None, None, None
             if is_tile(m - FLIP_LAG):
-                attn_bank = new_flip_bank()
-                flips.extend(
-                    flips_into(attn_bank, [attn[m - FLIP_LAG][:, j * P : (j + 1) * P] for j in range(PACK)])
-                )
+                attn_bank = flip_banks.tile([P, PACK, P], BF16, name="attn_bank", tag="flip_bank")
+                weave(behind, ATTN_FIRST, attn_flips(attn_bank, m - FLIP_LAG))
             if is_tile(m + Q_LEAD):
-                q_bank = new_flip_bank()
-                q_tile = q_raw[(m + Q_LEAD) // PAIR][:, (m + Q_LEAD) % PAIR, :]
-                flips.extend(flips_into(q_bank, [q_tile[:, c * P : (c + 1) * P] for c in range(CHUNKS)]))
+                q_bank = flip_banks.tile([P, GROUPS, P], F32, name="q_bank", tag="flip_bank")
+                weave(behind, Q_FIRST, word_flips(q_bank, q_raw[(m + Q_LEAD) // PAIR][:, (m + Q_LEAD) % PAIR, :]))
             head, steps_in = divmod(m + K_STRIDE * PACK, TILES_PER_HEAD)
             piece = steps_in // K_STRIDE
             if head < HEADS and piece < PACK and steps_in % K_STRIDE == 0:
-                k_bank = new_flip_bank()
-                flips.extend(
-                    flips_into(k_bank, [k_raw[(head, piece)][:, c * P : (c + 1) * P] for c in range(CHUNKS)])
-                )
+                k_bank = flip_banks.tile([P, GROUPS, P], F32, name="k_bank", tag="flip_bank")
+                weave(behind, K_FIRST, word_flips(k_bank, k_raw[(head, piece)][:]))
 
-            dots = multiply_qk(m, flips)
+            dots = multiply_qk(m, behind)
 
             if attn_bank is not None:
                 regroup_attn(m - FLIP_LAG, attn_bank)
             if q_bank is not None:
-                q_turned[m + Q_LEAD] = hand.tile([P, CHUNKS, P], BF16, name="q_turned")
-                nc.scalar.copy(out=q_turned[m + Q_LEAD][:], in_=q_bank[:])
+                q_turned[m + Q_LEAD] = hand.tile([P, GROUPS, PAIR * P], BF16, name="q_turned")
+                nc.scalar.copy(out=q_turned[m + Q_LEAD][:], in_=q_bank[:].bitcast(BF16))
+            normalise(m - 1)
+            quantise_v(m - 1)
             if k_bank is not None:
-                nc.scalar.copy(out=k_turned[head][:, :, piece * P : (piece + 1) * P], in_=k_bank[:])
+                nc.vector.tensor_copy(
+                    out=k_turned[head][:, :, piece * PAIR * P : (piece + 1) * PAIR * P], in_=k_bank[:].bitcast(BF16)
+                )
             regroup_v(m)
             square(m, dots)
 
-            multiply_mx(m - MX_LAG)
+            if m % 2 == 1:
+                multiply_mx(m - MX_LAG - 1)
+                multiply_mx(m - MX_LAG)

@@ -77,10 +77,9 @@ def tile_polynomialattn_t_kernel(tc, q, k, v, out):
             v_raw[h] = keep.tile([P, PACK, D], BF16, name="v_raw%d" % h)
             nc.sync.dma_start(out=v_raw[h][:], in_=v_heads[h])
 
-        for j in range(PACK - 1):
+        for j in range(PACK):
             load_k(0, j)
         load_q(0)
-        load_k(0, PACK - 1)
         load_q(1)
         load_v(0)
         load_q(2)
@@ -93,7 +92,7 @@ def tile_polynomialattn_t_kernel(tc, q, k, v, out):
 
         k_turned, v_codes, v_scales = {}, {}, {}
         for h in range(HEADS):
-            k_turned[h] = keep.tile([P, GROUPS, PAIR * T], BF16, name="k_turned%d" % h)
+            k_turned[h] = keep.tile([P, GROUPS, T], F32, name="k_turned%d" % h)
             v_codes[h] = keep.tile([P, D], U32, name="v_codes%d" % h, align_bytes=64)
             v_scales[h] = keep.tile([P, D], U8, name="v_scales%d" % h, align_bytes=64)
 
@@ -110,8 +109,18 @@ def tile_polynomialattn_t_kernel(tc, q, k, v, out):
             words = row_tile.bitcast(F32)
             return [(bank[:, g, :], words[:, g * P : (g + 1) * P], identity_words) for g in range(GROUPS)]
 
+        def k_flips(bank, head, u, g_pair):
+            flips = []
+            for g2 in range(PAIR):
+                g = PAIR * g_pair + g2
+                for e in range(PAIR):
+                    words = k_raw[(head, PAIR * u + e)][:].bitcast(F32)
+                    flips.append((bank[:, g2, e, :], words[:, g * P : (g + 1) * P], identity_words))
+            return flips
+
         def attn_flips(bank, m):
-            return [(bank[:, j, :], attn[m][:, j * P : (j + 1) * P], identity) for j in range(PACK)]
+            words = attn[m][:].bitcast(F32)
+            return [(bank[:, u, :], words[:, u * P : (u + 1) * P], identity_words) for u in range(PAIR)]
 
         def weave(behind, first, flips):
             for n, flip in enumerate(flips):
@@ -127,7 +136,7 @@ def tile_polynomialattn_t_kernel(tc, q, k, v, out):
                     nc.tensor.matmul(
                         out=dots[:],
                         lhsT=q_turned[m][:, g, e : PAIR * P : PAIR],
-                        rhs=k_turned[m // TILES_PER_HEAD][:, g, e : PAIR * T : PAIR],
+                        rhs=k_turned[m // TILES_PER_HEAD][:, g, :].bitcast(BF16)[:, e : PAIR * T : PAIR],
                         start=(n == 0),
                         stop=(n == MATMULS - 1),
                     )
@@ -153,8 +162,8 @@ def tile_polynomialattn_t_kernel(tc, q, k, v, out):
             nc.vector.tensor_scalar_mul(out=attn[m][:], in0=x[m][:], scalar1=inverse[:])
 
         def regroup_attn(m, bank):
-            attn_grouped[m] = hand.tile([P, P, PACK], BF16, name="attn_grouped", align_bytes=64)
-            nc.vector.tensor_copy(out=attn_grouped[m][:], in_=bank[:].rearrange("p j s -> p s j"))
+            attn_grouped[m] = hand.tile([P, P, PAIR], F32, name="attn_grouped", align_bytes=64)
+            nc.vector.tensor_copy(out=attn_grouped[m][:], in_=bank[:].rearrange("p u s -> p s u"))
 
         def quantise_attn(m):
             if not is_tile(m):
@@ -164,7 +173,7 @@ def tile_polynomialattn_t_kernel(tc, q, k, v, out):
             nc.vector.quantize_mx(
                 out=attn_codes[m][:].bitcast(FP8X4),
                 scales=attn_scales[m][:],
-                in_=attn_grouped[m][:].rearrange("p s j -> p (s j)"),
+                in_=attn_grouped[m][:].rearrange("p s u -> p (s u)").bitcast(BF16),
             )
 
         def regroup_v(n):
@@ -218,16 +227,17 @@ def tile_polynomialattn_t_kernel(tc, q, k, v, out):
             behind = [[] for n in range(MATMULS)]
             attn_bank, q_bank, k_bank = None, None, None
             if is_tile(m - FLIP_LAG):
-                attn_bank = flip_banks.tile([P, PACK, P], BF16, name="attn_bank", tag="flip_bank")
+                attn_bank = flip_banks.tile([P, PAIR, P], F32, name="attn_bank", tag="flip_bank")
                 weave(behind, ATTN_FIRST, attn_flips(attn_bank, m - FLIP_LAG))
             if is_tile(m + Q_LEAD):
                 q_bank = flip_banks.tile([P, GROUPS, P], F32, name="q_bank", tag="flip_bank")
                 weave(behind, Q_FIRST, word_flips(q_bank, q_raw[(m + Q_LEAD) // PAIR][:, (m + Q_LEAD) % PAIR, :]))
             head, steps_in = divmod(m + K_STRIDE * PACK, TILES_PER_HEAD)
-            piece = steps_in // K_STRIDE
-            if head < HEADS and piece < PACK and steps_in % K_STRIDE == 0:
-                k_bank = flip_banks.tile([P, GROUPS, P], F32, name="k_bank", tag="flip_bank")
-                weave(behind, K_FIRST, word_flips(k_bank, k_raw[(head, piece)][:]))
+            part = steps_in // K_STRIDE
+            k_u, k_g_pair = divmod(part, PAIR)
+            if head < HEADS and part < PACK and steps_in % K_STRIDE == 0:
+                k_bank = flip_banks.tile([P, PAIR, PAIR, P], F32, name="k_bank", tag="flip_bank")
+                weave(behind, K_FIRST, k_flips(k_bank, head, k_u, k_g_pair))
 
             dots = multiply_qk(m, behind)
 
@@ -240,7 +250,10 @@ def tile_polynomialattn_t_kernel(tc, q, k, v, out):
             quantise_v(m - 1)
             if k_bank is not None:
                 nc.vector.tensor_copy(
-                    out=k_turned[head][:, :, piece * PAIR * P : (piece + 1) * PAIR * P], in_=k_bank[:].bitcast(BF16)
+                    out=k_turned[head][
+                        :, PAIR * k_g_pair : PAIR * (k_g_pair + 1), k_u * PAIR * P : (k_u + 1) * PAIR * P
+                    ].rearrange("p g (n e) -> p g n e", e=PAIR),
+                    in_=k_bank[:].rearrange("p g e n -> p g n e"),
                 )
             regroup_v(m)
             square(m, dots)

@@ -31,6 +31,7 @@ K_STRIDE = 2
 FLIPS_PER_MATMUL = 2
 ATTN_FIRST, Q_FIRST, K_FIRST = 0, 2, 6
 WARM_MATMULS = 16
+WARM_BEHIND = 4
 
 FLOPS = 2 * 2 * HEADS * S * T * D
 
@@ -59,15 +60,22 @@ def tile_polynomialattn_t_kernel(tc, q, k, v, out):
         identity_words = keep.tile([P, P], F32, name="identity_words")
         masks.make_identity(nc, identity_words[:])
 
-        warm = dots_banks.tile([P, T], F32, name="dots")
-        for n in range(WARM_MATMULS):
-            nc.tensor.matmul(out=warm[:, :P], lhsT=identity[:], rhs=identity[:], start=True, stop=True)
+        def keep_warm(count):
+            warm = dots_banks.tile([P, T], F32, name="dots")
+            for n in range(count):
+                nc.tensor.matmul(out=warm[:, :P], lhsT=identity[:], rhs=identity[:], start=True, stop=True)
+
+        keep_warm(WARM_MATMULS)
 
         q_raw, k_raw, v_raw = {}, {}, {}
 
         def load_q(r):
             q_raw[r] = keep.tile([P, PAIR, D], BF16, name="q_raw%d" % r)
-            nc.sync.dma_start(out=q_raw[r][:], in_=q_pairs[r])
+            if r == 0:
+                for u in range(PAIR):
+                    nc.sync.dma_start(out=q_raw[r][:, u, :], in_=q_pairs[r][:, u, :])
+            else:
+                nc.sync.dma_start(out=q_raw[r][:], in_=q_pairs[r])
 
         def load_k(h, j):
             k_raw[(h, j)] = keep.tile([P, D], BF16, name="k_raw%d_%d" % (h, j))
@@ -236,10 +244,16 @@ def tile_polynomialattn_t_kernel(tc, q, k, v, out):
             part = steps_in // K_STRIDE
             k_u, k_g_pair = divmod(part, PAIR)
             if head < HEADS and part < PACK and steps_in % K_STRIDE == 0:
-                k_bank = flip_banks.tile([P, PAIR, PAIR, P], F32, name="k_bank", tag="flip_bank")
-                weave(behind, K_FIRST, k_flips(k_bank, head, k_u, k_g_pair))
+                if m < 0:
+                    k_bank = prod_banks.tile([P, PAIR, PAIR, P], F32, name="k_bank", tag="product")
+                    weave(behind, 0, k_flips(k_bank, head, k_u, k_g_pair))
+                else:
+                    k_bank = flip_banks.tile([P, PAIR, PAIR, P], F32, name="k_bank", tag="flip_bank")
+                    weave(behind, K_FIRST, k_flips(k_bank, head, k_u, k_g_pair))
 
             dots = multiply_qk(m, behind)
+            if m < 0 and any(behind):
+                keep_warm(WARM_BEHIND)
 
             if attn_bank is not None:
                 regroup_attn(m - FLIP_LAG, attn_bank)
@@ -249,7 +263,8 @@ def tile_polynomialattn_t_kernel(tc, q, k, v, out):
             normalise(m - 1)
             quantise_v(m - 1)
             if k_bank is not None:
-                nc.vector.tensor_copy(
+                copy_k = nc.scalar.copy if m < 0 and part % 2 == 0 else nc.vector.tensor_copy
+                copy_k(
                     out=k_turned[head][
                         :, PAIR * k_g_pair : PAIR * (k_g_pair + 1), k_u * PAIR * P : (k_u + 1) * PAIR * P
                     ].rearrange("p g (n e) -> p g n e", e=PAIR),

@@ -29,7 +29,7 @@ MX_LAG = 4
 OUT_LAG = 6
 K_STRIDE = 2
 FLIPS_PER_MATMUL = 2
-ATTN_FIRST, Q_FIRST, K_FIRST = 0, 2, 6
+ATTN_FIRST, Q_FIRST, K_FIRST = 4, 1, 6
 WARM_MATMULS = 16
 WARM_BEHIND = 4
 

@@ -23,19 +23,19 @@ TILES = HEADS * TILES_PER_HEAD
 MATMULS = GROUPS * PAIR
 
 Q_LEAD = 2
-FLIP_LAG = 3
-QUANT_LAG = 4
-MX_LAG = 4
-OUT_LAG = 6
+FLIP_LAG = 2
+QUANT_LAG = 3
+MX_LAG = 3
+OUT_LAG = 5
 K_STRIDE = 2
 FLIPS_PER_MATMUL = 2
 ATTN_FIRST, Q_FIRST, K_FIRST = 4, 1, 6
-WARM_MATMULS = 16
+WARM_MATMULS = 10
 WARM_BEHIND = 4
 
 FLOPS = 2 * 2 * HEADS * S * T * D
 
-assert T == PACK * P and K_STRIDE % 2 == 0 and MX_LAG % 2 == 0
+assert T == PACK * P and K_STRIDE % 2 == 0
 
 
 def tile_polynomialattn_t_kernel(tc, q, k, v, out):
@@ -49,6 +49,7 @@ def tile_polynomialattn_t_kernel(tc, q, k, v, out):
     with ExitStack() as ctx:
         keep = ctx.enter_context(tc.tile_pool(name="keep", bufs=1))
         hand = ctx.enter_context(tc.tile_pool(name="hand", bufs=4))
+        results = ctx.enter_context(tc.tile_pool(name="results", bufs=8))
         v_stage = ctx.enter_context(tc.tile_pool(name="v_stage", bufs=2))
         dots_banks = ctx.enter_context(tc.psum_pool(name="dots_banks", bufs=2))
         flip_banks = ctx.enter_context(tc.psum_pool(name="flip_banks", bufs=2))
@@ -71,11 +72,7 @@ def tile_polynomialattn_t_kernel(tc, q, k, v, out):
 
         def load_q(r):
             q_raw[r] = keep.tile([P, PAIR, D], BF16, name="q_raw%d" % r)
-            if r == 0:
-                for u in range(PAIR):
-                    nc.sync.dma_start(out=q_raw[r][:, u, :], in_=q_pairs[r][:, u, :])
-            else:
-                nc.sync.dma_start(out=q_raw[r][:], in_=q_pairs[r])
+            nc.sync.dma_start(out=q_raw[r][:], in_=q_pairs[r])
 
         def load_k(h, j):
             k_raw[(h, j)] = keep.tile([P, D], BF16, name="k_raw%d_%d" % (h, j))
@@ -85,9 +82,11 @@ def tile_polynomialattn_t_kernel(tc, q, k, v, out):
             v_raw[h] = keep.tile([P, PACK, D], BF16, name="v_raw%d" % h)
             nc.sync.dma_start(out=v_raw[h][:], in_=v_heads[h])
 
-        for j in range(PACK):
-            load_k(0, j)
-        load_q(0)
+        q_raw[0] = keep.tile([P, PAIR, D], BF16, name="q_raw0")
+        for u in range(PAIR):
+            for j in range(PAIR):
+                load_k(0, PAIR * u + j)
+            nc.sync.dma_start(out=q_raw[0][:, u, :], in_=q_pairs[0][:, u, :])
         load_q(1)
         load_v(0)
         load_q(2)
@@ -110,8 +109,7 @@ def tile_polynomialattn_t_kernel(tc, q, k, v, out):
         def is_tile(m):
             return 0 <= m < TILES
 
-        def is_v_half(n):
-            return 0 <= n < HEADS * HALVES
+        v_halves = {1: (0, 1), 9: (2,), 11: (3,)}
 
         def word_flips(bank, row_tile):
             words = row_tile.bitcast(F32)
@@ -119,9 +117,9 @@ def tile_polynomialattn_t_kernel(tc, q, k, v, out):
 
         def k_flips(bank, head, u, g_pair):
             flips = []
-            for g2 in range(PAIR):
-                g = PAIR * g_pair + g2
-                for e in range(PAIR):
+            for e in range(PAIR):
+                for g2 in range(PAIR):
+                    g = PAIR * g_pair + g2
                     words = k_raw[(head, PAIR * u + e)][:].bitcast(F32)
                     flips.append((bank[:, g2, e, :], words[:, g * P : (g + 1) * P], identity_words))
             return flips
@@ -134,27 +132,26 @@ def tile_polynomialattn_t_kernel(tc, q, k, v, out):
             for n, flip in enumerate(flips):
                 behind[first + n // FLIPS_PER_MATMUL].append(flip)
 
-        def multiply_qk(m, behind):
-            dots = None
-            if is_tile(m):
-                dots = dots_banks.tile([P, T], F32, name="dots")
+        def issue_flips(flips):
+            for target, block, one in flips:
+                nc.tensor.transpose(target, block, one[:])
+
+        def multiply_qk(m, dots, keys, behind, mx_behind=None, mx_tiles=()):
             for n in range(MATMULS):
                 g, e = divmod(n, PAIR)
-                if is_tile(m):
-                    nc.tensor.matmul(
-                        out=dots[:],
-                        lhsT=q_turned[m][:, g, e : PAIR * P : PAIR],
-                        rhs=k_turned[m // TILES_PER_HEAD][:, g, :].bitcast(BF16)[:, e : PAIR * T : PAIR],
-                        start=(n == 0),
-                        stop=(n == MATMULS - 1),
-                    )
-                for target, block, one in behind[n]:
-                    nc.tensor.transpose(target, block, one[:])
-            return dots
+                nc.tensor.matmul(
+                    out=dots[:, keys],
+                    lhsT=q_turned[m][:, g, :].bitcast(BF16)[:, e : PAIR * P : PAIR],
+                    rhs=k_turned[m // TILES_PER_HEAD][:, g, keys].bitcast(BF16)[:, e : PAIR * (keys.stop - keys.start) : PAIR],
+                    start=(n == 0),
+                    stop=(n == MATMULS - 1),
+                )
+                issue_flips(behind[n])
+                if n == mx_behind:
+                    for late in mx_tiles:
+                        multiply_mx(late, prod_banks, "product")
 
         def square(m, dots):
-            if not is_tile(m):
-                return
             x[m] = hand.tile([P, T], F32, name="x")
             row_sum[m] = hand.tile([P, 1], F32, name="row_sum")
             nc.scalar.activation(out=x[m][:], in_=dots[:], func=SQUARE, accum_out=row_sum[m][:])
@@ -168,6 +165,18 @@ def tile_polynomialattn_t_kernel(tc, q, k, v, out):
             nc.vector.reciprocal(out=inverse[:], in_=denom[:])
             attn[m] = hand.tile([P, T], BF16, name="attn")
             nc.vector.tensor_scalar_mul(out=attn[m][:], in0=x[m][:], scalar1=inverse[:])
+
+        def take_q(m, bank):
+            q_turned[m] = hand.tile([P, GROUPS, P], F32, name="q_turned")
+            nc.scalar.copy(out=q_turned[m][:], in_=bank[:])
+
+        def take_k(copy, head, u, g_pair, bank):
+            copy(
+                out=k_turned[head][
+                    :, PAIR * g_pair : PAIR * (g_pair + 1), u * PAIR * P : (u + 1) * PAIR * P
+                ].rearrange("p g (n e) -> p g n e", e=PAIR),
+                in_=bank[:].rearrange("p g e n -> p g n e"),
+            )
 
         def regroup_attn(m, bank):
             attn_grouped[m] = hand.tile([P, P, PAIR], F32, name="attn_grouped", align_bytes=64)
@@ -185,8 +194,6 @@ def tile_polynomialattn_t_kernel(tc, q, k, v, out):
             )
 
         def regroup_v(n):
-            if not is_v_half(n):
-                return
             cols = slice((n % HALVES) * BANK, (n % HALVES + 1) * BANK)
             v_grouped[n] = v_stage.tile([P, BANK, PACK], BF16, name="v_grouped", align_bytes=64)
             nc.vector.tensor_copy(
@@ -194,8 +201,6 @@ def tile_polynomialattn_t_kernel(tc, q, k, v, out):
             )
 
         def quantise_v(n):
-            if not is_v_half(n):
-                return
             cols = slice((n % HALVES) * BANK, (n % HALVES + 1) * BANK)
             nc.vector.quantize_mx(
                 out=v_codes[n // HALVES][:, cols].bitcast(FP8X4),
@@ -203,13 +208,13 @@ def tile_polynomialattn_t_kernel(tc, q, k, v, out):
                 in_=v_grouped[n][:].rearrange("p d j -> p (d j)"),
             )
 
-        def multiply_mx(m):
+        def multiply_mx(m, banks, tag):
             if not is_tile(m):
                 return
             h = m // TILES_PER_HEAD
             for half in range(HALVES):
                 cols = slice(half * BANK, (half + 1) * BANK)
-                products[(m, half)] = prod_banks.tile([P, BANK], F32, name="product")
+                products[(m, half)] = banks.tile([P, BANK], F32, name="product", tag=tag)
                 nc.tensor.matmul_mx(
                     out=products[(m, half)][:],
                     lhsT=attn_codes[m][:].bitcast(FP8X4),
@@ -223,56 +228,115 @@ def tile_polynomialattn_t_kernel(tc, q, k, v, out):
         def store_products(m):
             if not is_tile(m):
                 return
-            result = hand.tile([P, D], F32, name="result")
+            result = results.tile([P, D], F32, name="result")
             nc.scalar.copy(out=result[:, :BANK], in_=products[(m, 0)][:])
             nc.vector.tensor_copy(out=result[:, BANK:], in_=products[(m, 1)][:])
             nc.sync.dma_start(out=out_pairs[m // PAIR][:, m % PAIR, :], in_=result[:])
 
-        for m in range(-K_STRIDE * PACK, TILES + OUT_LAG):
+        def store_halves(m, copy_second):
+            result = results.tile([P, D], F32, name="result")
+            for half, copy in ((0, nc.scalar.copy), (1, copy_second)):
+                cols = slice(half * BANK, (half + 1) * BANK)
+                copy(out=result[:, cols], in_=products[(m, half)][:])
+                nc.sync.dma_start(out=out_pairs[m // PAIR][:, m % PAIR, cols], in_=result[:, cols])
+
+        def q_words(m):
+            return q_raw[m // PAIR][:, m % PAIR, :]
+
+        def no_flips():
+            return [[] for n in range(MATMULS)]
+
+        first_k = [prod_banks.tile([P, PAIR, PAIR, P], F32, name="k_bank", tag="product") for part in range(PACK)]
+        k_parts = [k_flips(first_k[part], 0, *divmod(part, PAIR)) for part in range(PACK)]
+        def flip_piece(piece):
+            u, e = divmod(piece, PAIR)
+            for part in (PAIR * u, PAIR * u + 1):
+                issue_flips(k_parts[part][PAIR * e : PAIR * (e + 1)])
+
+        flip_piece(0)
+        flip_piece(1)
+        take_k(nc.scalar.copy, 0, 0, 0, first_k[0])
+        take_k(nc.vector.tensor_copy, 0, 0, 1, first_k[1])
+        q_bank = flip_banks.tile([P, GROUPS, P], F32, name="q_bank", tag="flip_bank")
+        issue_flips(word_flips(q_bank, q_words(0)))
+        take_q(0, q_bank)
+        keep_warm(WARM_BEHIND)
+        flip_piece(2)
+        flip_piece(3)
+
+        dots = dots_banks.tile([P, T], F32, name="dots")
+        take_k(nc.vector.tensor_copy, 0, 1, 0, first_k[2])
+        take_k(nc.scalar.copy, 0, 1, 1, first_k[3])
+        multiply_qk(0, dots, slice(0, T // 2), no_flips())
+        behind = no_flips()
+        q_bank = flip_banks.tile([P, GROUPS, P], F32, name="q_bank", tag="flip_bank")
+        weave(behind, Q_FIRST, word_flips(q_bank, q_words(1)))
+        multiply_qk(0, dots, slice(T // 2, T), behind)
+        take_q(1, q_bank)
+        square(0, dots)
+
+        last = TILES - 1
+        for m in range(1, TILES):
             quantise_attn(m - QUANT_LAG)
             store_products(m - OUT_LAG)
 
-            behind = [[] for n in range(MATMULS)]
-            attn_bank, q_bank, k_bank = None, None, None
+            behind = no_flips()
+            attn_bank, k_bank, q_banks = None, None, {}
             if is_tile(m - FLIP_LAG):
                 attn_bank = flip_banks.tile([P, PAIR, P], F32, name="attn_bank", tag="flip_bank")
                 weave(behind, ATTN_FIRST, attn_flips(attn_bank, m - FLIP_LAG))
-            if is_tile(m + Q_LEAD):
-                q_bank = flip_banks.tile([P, GROUPS, P], F32, name="q_bank", tag="flip_bank")
-                weave(behind, Q_FIRST, word_flips(q_bank, q_raw[(m + Q_LEAD) // PAIR][:, (m + Q_LEAD) % PAIR, :]))
-            head, steps_in = divmod(m + K_STRIDE * PACK, TILES_PER_HEAD)
-            part = steps_in // K_STRIDE
+            for first, n in ((Q_FIRST, 2), (ATTN_FIRST, 3)) if m == 1 else ((Q_FIRST, m + Q_LEAD),):
+                if is_tile(n):
+                    q_banks[n] = flip_banks.tile([P, GROUPS, P], F32, name="q_bank", tag="flip_bank")
+                    weave(behind, first, word_flips(q_banks[n], q_words(n)))
+            part, odd = divmod(m - TILES_PER_HEAD + K_STRIDE * PACK, K_STRIDE)
             k_u, k_g_pair = divmod(part, PAIR)
-            if head < HEADS and part < PACK and steps_in % K_STRIDE == 0:
-                if m < 0:
-                    k_bank = prod_banks.tile([P, PAIR, PAIR, P], F32, name="k_bank", tag="product")
-                    weave(behind, 0, k_flips(k_bank, head, k_u, k_g_pair))
-                else:
-                    k_bank = flip_banks.tile([P, PAIR, PAIR, P], F32, name="k_bank", tag="flip_bank")
-                    weave(behind, K_FIRST, k_flips(k_bank, head, k_u, k_g_pair))
+            if 0 <= part < PACK and odd == 0:
+                k_bank = flip_banks.tile([P, PAIR, PAIR, P], F32, name="k_bank", tag="flip_bank")
+                weave(behind, K_FIRST, k_flips(k_bank, 1, k_u, k_g_pair))
 
-            dots = multiply_qk(m, behind)
-            if m < 0 and any(behind):
-                keep_warm(WARM_BEHIND)
+            dots = dots_banks.tile([P, T], F32, name="dots")
+            if m < last:
+                multiply_qk(m, dots, slice(0, T), behind)
+            else:
+                multiply_qk(m, dots, slice(0, T), behind, 2, (last - MX_LAG - 1, last - MX_LAG))
 
+            normalise(m - 1)
+            if m == last:
+                store_halves(last - 4, nc.vector.tensor_copy)
+                store_halves(last - 3, nc.vector.tensor_copy)
             if attn_bank is not None:
                 regroup_attn(m - FLIP_LAG, attn_bank)
-            if q_bank is not None:
-                q_turned[m + Q_LEAD] = hand.tile([P, GROUPS, PAIR * P], BF16, name="q_turned")
-                nc.scalar.copy(out=q_turned[m + Q_LEAD][:], in_=q_bank[:].bitcast(BF16))
-            normalise(m - 1)
-            quantise_v(m - 1)
+            for n in q_banks:
+                take_q(n, q_banks[n])
+            for n in v_halves.get(m - 1, ()):
+                quantise_v(n)
             if k_bank is not None:
-                copy_k = nc.scalar.copy if m < 0 and part % 2 == 0 else nc.vector.tensor_copy
-                copy_k(
-                    out=k_turned[head][
-                        :, PAIR * k_g_pair : PAIR * (k_g_pair + 1), k_u * PAIR * P : (k_u + 1) * PAIR * P
-                    ].rearrange("p g (n e) -> p g n e", e=PAIR),
-                    in_=k_bank[:].rearrange("p g e n -> p g n e"),
-                )
-            regroup_v(m)
+                take_k(nc.vector.tensor_copy, 1, k_u, k_g_pair, k_bank)
+            for n in v_halves.get(m, ()):
+                regroup_v(n)
             square(m, dots)
 
-            if m % 2 == 1:
-                multiply_mx(m - MX_LAG - 1)
-                multiply_mx(m - MX_LAG)
+            if m % 2 == 1 and m < TILES - 1:
+                multiply_mx(m - MX_LAG - 1, prod_banks, "product")
+                multiply_mx(m - MX_LAG, prod_banks, "product")
+
+        def flip_attn(m):
+            attn_bank = flip_banks.tile([P, PAIR, P], F32, name="attn_bank", tag="flip_bank")
+            issue_flips(attn_flips(attn_bank, m))
+            return attn_bank
+
+        bank_before_last = flip_attn(last - 1)
+        quantise_attn(last - 2)
+        multiply_mx(last - 2, prod_banks, "product")
+        regroup_attn(last - 1, bank_before_last)
+        normalise(last)
+        quantise_attn(last - 1)
+        bank_last = flip_attn(last)
+        multiply_mx(last - 1, prod_banks, "product")
+        store_halves(last - 2, nc.scalar.copy)
+        regroup_attn(last, bank_last)
+        quantise_attn(last)
+        multiply_mx(last, dots_banks, "dots")
+        for m in range(last - 1, TILES):
+            store_halves(m, nc.vector.tensor_copy)

@@ -30,8 +30,8 @@ OUT_LAG = 5
 K_STRIDE = 2
 FLIPS_PER_MATMUL = 2
 ATTN_FIRST, Q_FIRST, K_FIRST = 4, 1, 6
-WARM_MATMULS = 10
-WARM_BEHIND = 4
+WARM_MATMULS = 16
+WARM_BEHIND = 3
 
 FLOPS = 2 * 2 * HEADS * S * T * D
 
@@ -254,7 +254,9 @@ def tile_polynomialattn_t_kernel(tc, q, k, v, out):
                 issue_flips(k_parts[part][PAIR * e : PAIR * (e + 1)])
 
         flip_piece(0)
+        keep_warm(WARM_BEHIND)
         flip_piece(1)
+        keep_warm(WARM_BEHIND)
         take_k(nc.scalar.copy, 0, 0, 0, first_k[0])
         take_k(nc.vector.tensor_copy, 0, 0, 1, first_k[1])
         q_bank = flip_banks.tile([P, GROUPS, P], F32, name="q_bank", tag="flip_bank")
@@ -262,7 +264,9 @@ def tile_polynomialattn_t_kernel(tc, q, k, v, out):
         take_q(0, q_bank)
         keep_warm(WARM_BEHIND)
         flip_piece(2)
+        keep_warm(WARM_BEHIND)
         flip_piece(3)
+        keep_warm(WARM_BEHIND)
 
         dots = dots_banks.tile([P, T], F32, name="dots")
         take_k(nc.vector.tensor_copy, 0, 1, 0, first_k[2])

@@ -9,6 +9,7 @@ U32 = mybir.dt.uint32
 U8 = mybir.dt.uint8
 FP8X4 = mybir.dt.float8_e4m3fn_x4
 SQUARE = mybir.ActivationFunctionType.Square
+ADD, MAX = mybir.AluOpType.add, mybir.AluOpType.max
 
 P = 128
 HEADS, S, T, D = 2, 2048, 512, 1024
@@ -84,9 +85,9 @@ def tile_polynomialattn_t_kernel(tc, q, k, v, out):
 
         q_raw[0] = keep.tile([P, PAIR, D], BF16, name="q_raw0")
         for u in range(PAIR):
+            nc.sync.dma_start(out=q_raw[0][:, u, :], in_=q_pairs[0][:, u, :])
             for j in range(PAIR):
                 load_k(0, PAIR * u + j)
-            nc.sync.dma_start(out=q_raw[0][:, u, :], in_=q_pairs[0][:, u, :])
         load_q(1)
         load_v(0)
         load_q(2)
@@ -105,6 +106,8 @@ def tile_polynomialattn_t_kernel(tc, q, k, v, out):
 
         q_turned, x, row_sum, attn, attn_grouped, attn_codes, attn_scales = {}, {}, {}, {}, {}, {}, {}
         v_grouped, products = {}, {}
+
+        last = TILES - 1
 
         def is_tile(m):
             return 0 <= m < TILES
@@ -136,20 +139,18 @@ def tile_polynomialattn_t_kernel(tc, q, k, v, out):
             for target, block, one in flips:
                 nc.tensor.transpose(target, block, one[:])
 
-        def multiply_qk(m, dots, keys, behind, mx_behind=None, mx_tiles=()):
+        def multiply_qk(m, dots, keys, behind, to=None):
+            to = keys if to is None else to
             for n in range(MATMULS):
                 g, e = divmod(n, PAIR)
                 nc.tensor.matmul(
-                    out=dots[:, keys],
+                    out=dots[:, to],
                     lhsT=q_turned[m][:, g, :].bitcast(BF16)[:, e : PAIR * P : PAIR],
                     rhs=k_turned[m // TILES_PER_HEAD][:, g, keys].bitcast(BF16)[:, e : PAIR * (keys.stop - keys.start) : PAIR],
                     start=(n == 0),
                     stop=(n == MATMULS - 1),
                 )
                 issue_flips(behind[n])
-                if n == mx_behind:
-                    for late in mx_tiles:
-                        multiply_mx(late, prod_banks, "product")
 
         def square(m, dots):
             x[m] = hand.tile([P, T], F32, name="x")
@@ -166,16 +167,17 @@ def tile_polynomialattn_t_kernel(tc, q, k, v, out):
             attn[m] = hand.tile([P, T], BF16, name="attn")
             nc.vector.tensor_scalar_mul(out=attn[m][:], in0=x[m][:], scalar1=inverse[:])
 
-        def take_q(m, bank):
+        def take_q(copy, m, bank):
             q_turned[m] = hand.tile([P, GROUPS, P], F32, name="q_turned")
-            nc.scalar.copy(out=q_turned[m][:], in_=bank[:])
+            copy(out=q_turned[m][:], in_=bank[:])
 
-        def take_k(copy, head, u, g_pair, bank):
+        def take_k(copy, head, u, g_pair, bank, g2=None):
+            groups = slice(0, PAIR) if g2 is None else slice(g2, g2 + 1)
             copy(
                 out=k_turned[head][
-                    :, PAIR * g_pair : PAIR * (g_pair + 1), u * PAIR * P : (u + 1) * PAIR * P
+                    :, PAIR * g_pair + groups.start : PAIR * g_pair + groups.stop, u * PAIR * P : (u + 1) * PAIR * P
                 ].rearrange("p g (n e) -> p g n e", e=PAIR),
-                in_=bank[:].rearrange("p g e n -> p g n e"),
+                in_=bank[:, groups, :, :].rearrange("p g e n -> p g n e"),
             )
 
         def regroup_attn(m, bank):
@@ -208,15 +210,15 @@ def tile_polynomialattn_t_kernel(tc, q, k, v, out):
                 in_=v_grouped[n][:].rearrange("p d j -> p (d j)"),
             )
 
-        def multiply_mx(m, banks, tag):
+        def multiply_mx(m, banks=prod_banks, tag="product", pieces=range(HALVES), width=BANK):
             if not is_tile(m):
                 return
             h = m // TILES_PER_HEAD
-            for half in range(HALVES):
-                cols = slice(half * BANK, (half + 1) * BANK)
-                products[(m, half)] = banks.tile([P, BANK], F32, name="product", tag=tag)
+            for piece in pieces:
+                cols = slice(piece * width, (piece + 1) * width)
+                products[(m, piece)] = banks.tile([P, BANK], F32, name="product", tag=tag)
                 nc.tensor.matmul_mx(
-                    out=products[(m, half)][:],
+                    out=products[(m, piece)][:, :width],
                     lhsT=attn_codes[m][:].bitcast(FP8X4),
                     lhsT_scale=attn_scales[m][:],
                     rhs=v_codes[h][:, cols].bitcast(FP8X4),
@@ -233,12 +235,10 @@ def tile_polynomialattn_t_kernel(tc, q, k, v, out):
             nc.vector.tensor_copy(out=result[:, BANK:], in_=products[(m, 1)][:])
             nc.sync.dma_start(out=out_pairs[m // PAIR][:, m % PAIR, :], in_=result[:])
 
-        def store_halves(m, copy_second):
-            result = results.tile([P, D], F32, name="result")
-            for half, copy in ((0, nc.scalar.copy), (1, copy_second)):
-                cols = slice(half * BANK, (half + 1) * BANK)
-                copy(out=result[:, cols], in_=products[(m, half)][:])
-                nc.sync.dma_start(out=out_pairs[m // PAIR][:, m % PAIR, cols], in_=result[:, cols])
+        def store_piece(m, copy, piece, width=BANK):
+            result = results.tile([P, width], F32, name="result_piece%d" % width)
+            copy(out=result[:], in_=products[(m, piece)][:, :width])
+            nc.sync.dma_start(out=out_pairs[m // PAIR][:, m % PAIR, piece * width : (piece + 1) * width], in_=result[:])
 
         def q_words(m):
             return q_raw[m // PAIR][:, m % PAIR, :]
@@ -253,46 +253,57 @@ def tile_polynomialattn_t_kernel(tc, q, k, v, out):
             for part in (PAIR * u, PAIR * u + 1):
                 issue_flips(k_parts[part][PAIR * e : PAIR * (e + 1)])
 
-        flip_piece(0)
-        keep_warm(WARM_BEHIND)
-        flip_piece(1)
-        keep_warm(WARM_BEHIND)
-        take_k(nc.scalar.copy, 0, 0, 0, first_k[0])
-        take_k(nc.vector.tensor_copy, 0, 0, 1, first_k[1])
-        q_bank = flip_banks.tile([P, GROUPS, P], F32, name="q_bank", tag="flip_bank")
-        issue_flips(word_flips(q_bank, q_words(0)))
-        take_q(0, q_bank)
-        keep_warm(WARM_BEHIND)
-        flip_piece(2)
-        keep_warm(WARM_BEHIND)
-        flip_piece(3)
-        keep_warm(WARM_BEHIND)
+        def flip_q(m):
+            bank = flip_banks.tile([P, GROUPS, P], F32, name="q_bank", tag="flip_bank")
+            return bank, word_flips(bank, q_words(m))
 
-        dots = dots_banks.tile([P, T], F32, name="dots")
+        def start_q(copy, m):
+            q_bank, flips = flip_q(m)
+            issue_flips(flips)
+            keep_warm(WARM_BEHIND)
+            take_q(copy, m, q_bank)
+
+        start_q(nc.scalar.copy, 0)
+        for piece in range(PAIR):
+            flip_piece(piece)
+            keep_warm(WARM_BEHIND)
+        for g2 in range(PAIR):
+            take_k(nc.scalar.copy, 0, 0, 0, first_k[0], g2)
+            take_k(nc.vector.tensor_copy, 0, 0, 1, first_k[1], g2)
+        start_q(nc.vector.tensor_copy, 1)
+
+        first_dots = [dots_banks.tile([P, T], F32, name="dots") for m in range(PAIR)]
+        behind = no_flips()
+        for part in (PAIR, PAIR + 1):
+            weave(behind, 1 + 3 * (part - PAIR), k_parts[part][:PAIR])
+            weave(behind, 3 + 3 * (part - PAIR), k_parts[part][PAIR:])
+        multiply_qk(0, first_dots[0], slice(0, T // 2), behind)
         take_k(nc.vector.tensor_copy, 0, 1, 0, first_k[2])
         take_k(nc.scalar.copy, 0, 1, 1, first_k[3])
-        multiply_qk(0, dots, slice(0, T // 2), no_flips())
-        behind = no_flips()
-        q_bank = flip_banks.tile([P, GROUPS, P], F32, name="q_bank", tag="flip_bank")
-        weave(behind, Q_FIRST, word_flips(q_bank, q_words(1)))
-        multiply_qk(0, dots, slice(T // 2, T), behind)
-        take_q(1, q_bank)
-        square(0, dots)
+        multiply_qk(1, first_dots[1], slice(0, T // 2), no_flips())
+        for m in range(PAIR):
+            behind = no_flips()
+            q_bank, flips = flip_q(m + Q_LEAD)
+            weave(behind, Q_FIRST, flips)
+            multiply_qk(m, first_dots[m], slice(T // 2, T), behind)
+            take_q(nc.scalar.copy, m + Q_LEAD, q_bank)
+            square(m, first_dots[m])
+        regroup_v(v_halves[1][0])
+        normalise(0)
+        regroup_v(v_halves[1][1])
 
-        last = TILES - 1
-        for m in range(1, TILES):
+        for m in range(PAIR, last):
             quantise_attn(m - QUANT_LAG)
             store_products(m - OUT_LAG)
 
             behind = no_flips()
-            attn_bank, k_bank, q_banks = None, None, {}
+            attn_bank, k_bank, q_bank = None, None, None
             if is_tile(m - FLIP_LAG):
                 attn_bank = flip_banks.tile([P, PAIR, P], F32, name="attn_bank", tag="flip_bank")
                 weave(behind, ATTN_FIRST, attn_flips(attn_bank, m - FLIP_LAG))
-            for first, n in ((Q_FIRST, 2), (ATTN_FIRST, 3)) if m == 1 else ((Q_FIRST, m + Q_LEAD),):
-                if is_tile(n):
-                    q_banks[n] = flip_banks.tile([P, GROUPS, P], F32, name="q_bank", tag="flip_bank")
-                    weave(behind, first, word_flips(q_banks[n], q_words(n)))
+            if is_tile(m + Q_LEAD):
+                q_bank, flips = flip_q(m + Q_LEAD)
+                weave(behind, Q_FIRST, flips)
             part, odd = divmod(m - TILES_PER_HEAD + K_STRIDE * PACK, K_STRIDE)
             k_u, k_g_pair = divmod(part, PAIR)
             if 0 <= part < PACK and odd == 0:
@@ -300,19 +311,13 @@ def tile_polynomialattn_t_kernel(tc, q, k, v, out):
                 weave(behind, K_FIRST, k_flips(k_bank, 1, k_u, k_g_pair))
 
             dots = dots_banks.tile([P, T], F32, name="dots")
-            if m < last:
-                multiply_qk(m, dots, slice(0, T), behind)
-            else:
-                multiply_qk(m, dots, slice(0, T), behind, 2, (last - MX_LAG - 1, last - MX_LAG))
+            multiply_qk(m, dots, slice(0, T), behind)
 
             normalise(m - 1)
-            if m == last:
-                store_halves(last - 4, nc.vector.tensor_copy)
-                store_halves(last - 3, nc.vector.tensor_copy)
             if attn_bank is not None:
                 regroup_attn(m - FLIP_LAG, attn_bank)
-            for n in q_banks:
-                take_q(n, q_banks[n])
+            if q_bank is not None:
+                take_q(nc.scalar.copy, m + Q_LEAD, q_bank)
             for n in v_halves.get(m - 1, ()):
                 quantise_v(n)
             if k_bank is not None:
@@ -321,26 +326,69 @@ def tile_polynomialattn_t_kernel(tc, q, k, v, out):
                 regroup_v(n)
             square(m, dots)
 
-            if m % 2 == 1 and m < TILES - 1:
-                multiply_mx(m - MX_LAG - 1, prod_banks, "product")
-                multiply_mx(m - MX_LAG, prod_banks, "product")
+            if m % 2 == 1:
+                multiply_mx(m - MX_LAG - 1)
+                multiply_mx(m - MX_LAG)
 
-        def flip_attn(m):
-            attn_bank = flip_banks.tile([P, PAIR, P], F32, name="attn_bank", tag="flip_bank")
-            issue_flips(attn_flips(attn_bank, m))
-            return attn_bank
+        quantise_attn(last - QUANT_LAG)
+        store_products(last - OUT_LAG)
+        x[last] = hand.tile([P, T], F32, name="x")
+        half_sums = hand.tile([P, PAIR], F32, name="half_sums")
 
-        bank_before_last = flip_attn(last - 1)
+        def multiply_half(half, attn_tile):
+            bank = flip_banks.tile([P, PAIR, P], F32, name="attn_bank", tag="flip_bank")
+            behind = no_flips()
+            weave(behind, 2, attn_flips(bank, attn_tile))
+            dots = dots_banks.tile([P, T], F32, name="dots")
+            multiply_qk(last, dots, slice(half * T // 2, (half + 1) * T // 2), behind, to=slice(0, T // 2))
+            return dots, bank
+
+        def square_half(half, dots):
+            nc.scalar.activation(
+                out=x[last][:, half * T // 2 : (half + 1) * T // 2],
+                in_=dots[:, : T // 2],
+                func=SQUARE,
+                accum_out=half_sums[:, half : half + 1],
+            )
+
+        dots, bank = multiply_half(0, last - 2)
+        square_half(0, dots)
+        multiply_mx(last - 4)
+        multiply_mx(last - 3)
+        normalise(last - 1)
+        regroup_attn(last - 2, bank)
+        store_piece(last - 4, nc.scalar.copy, 0)
+        store_piece(last - 4, nc.vector.tensor_copy, 1)
         quantise_attn(last - 2)
-        multiply_mx(last - 2, prod_banks, "product")
-        regroup_attn(last - 1, bank_before_last)
-        normalise(last)
+        store_piece(last - 3, nc.scalar.copy, 0)
+        store_piece(last - 3, nc.vector.tensor_copy, 1)
+        dots, bank = multiply_half(1, last - 1)
+        square_half(1, dots)
+        regroup_attn(last - 1, bank)
         quantise_attn(last - 1)
-        bank_last = flip_attn(last)
-        multiply_mx(last - 1, prod_banks, "product")
-        store_halves(last - 2, nc.scalar.copy)
-        regroup_attn(last, bank_last)
+        multiply_mx(last - 2)
+        multiply_mx(last - 1)
+
+        denom = hand.tile([P, 1], F32, name="denom")
+        nc.vector.tensor_scalar(
+            out=denom[:], in0=half_sums[:, 0:1], scalar1=half_sums[:, 1:2], scalar2=EPS, op0=ADD, op1=MAX
+        )
+        inverse = hand.tile([P, 1], F32, name="inverse")
+        nc.vector.reciprocal(out=inverse[:], in_=denom[:])
+        attn[last] = hand.tile([P, T], BF16, name="attn")
+        bank = flip_banks.tile([P, PAIR, P], F32, name="attn_bank", tag="flip_bank")
+        for half, flip in enumerate(attn_flips(bank, last)):
+            keys = slice(half * T // 2, (half + 1) * T // 2)
+            nc.vector.tensor_scalar_mul(out=attn[last][:, keys], in0=x[last][:, keys], scalar1=inverse[:])
+            issue_flips([flip])
+        store_piece(last - 2, nc.scalar.copy, 0)
+        store_piece(last - 2, nc.vector.tensor_copy, 1)
+        regroup_attn(last, bank)
         quantise_attn(last)
-        multiply_mx(last, dots_banks, "dots")
-        for m in range(last - 1, TILES):
-            store_halves(m, nc.vector.tensor_copy)
+        store_piece(last - 1, nc.scalar.copy, 0)
+        store_piece(last - 1, nc.scalar.copy, 1)
+        quarter = BANK // 2
+        multiply_mx(last, dots_banks, "dots", range(0, 2), quarter)
+        multiply_mx(last, prod_banks, "product", range(2, 4), quarter)
+        for piece in range(4):
+            store_piece(last, nc.vector.tensor_copy if piece % 2 else nc.scalar.copy, piece, quarter)

@@ -31,6 +31,8 @@ OUT_LAG = 5
 K_STRIDE = 2
 FLIPS_PER_MATMUL = 2
 ATTN_FIRST, Q_FIRST, K_FIRST = 4, 1, 6
+PART_K = {4: (0, 0), 5: (0, 1), 6: (0, 2), 7: (0, 3), 13: (1, 0), 15: (1, 1), 16: (1, 2), 17: (1, 3)}
+PARTED_FROM = (8, 18)
 WARM_MATMULS = 16
 WARM_BEHIND = 3
 
@@ -98,9 +100,10 @@ def tile_polynomialattn_t_kernel(tc, q, k, v, out):
         for r in range(4, TILES // PAIR):
             load_q(r)
 
-        k_turned, v_codes, v_scales = {}, {}, {}
+        k_turned, k_parted, v_codes, v_scales = {}, {}, {}, {}
         for h in range(HEADS):
             k_turned[h] = keep.tile([P, GROUPS, T], F32, name="k_turned%d" % h)
+            k_parted[h] = keep.tile([P, GROUPS, PAIR, T], BF16, name="k_parted%d" % h)
             v_codes[h] = keep.tile([P, D], U32, name="v_codes%d" % h, align_bytes=64)
             v_scales[h] = keep.tile([P, D], U8, name="v_scales%d" % h, align_bytes=64)
 
@@ -143,10 +146,15 @@ def tile_polynomialattn_t_kernel(tc, q, k, v, out):
             to = keys if to is None else to
             for n in range(MATMULS):
                 g, e = divmod(n, PAIR)
+                head = m // TILES_PER_HEAD
+                if m >= PARTED_FROM[head]:
+                    k_part = k_parted[head][:, g, e, keys]
+                else:
+                    k_part = k_turned[head][:, g, keys].bitcast(BF16)[:, e : PAIR * (keys.stop - keys.start) : PAIR]
                 nc.tensor.matmul(
                     out=dots[:, to],
                     lhsT=q_turned[m][:, g, :].bitcast(BF16)[:, e : PAIR * P : PAIR],
-                    rhs=k_turned[m // TILES_PER_HEAD][:, g, keys].bitcast(BF16)[:, e : PAIR * (keys.stop - keys.start) : PAIR],
+                    rhs=k_part,
                     start=(n == 0),
                     stop=(n == MATMULS - 1),
                 )
@@ -178,6 +186,12 @@ def tile_polynomialattn_t_kernel(tc, q, k, v, out):
                     :, PAIR * g_pair + groups.start : PAIR * g_pair + groups.stop, u * PAIR * P : (u + 1) * PAIR * P
                 ].rearrange("p g (n e) -> p g n e", e=PAIR),
                 in_=bank[:, groups, :, :].rearrange("p g e n -> p g n e"),
+            )
+
+        def part_k(head, g):
+            nc.vector.tensor_copy(
+                out=k_parted[head][:, g, :, :],
+                in_=k_turned[head][:, g, :].bitcast(BF16).rearrange("p (c e) -> p e c", e=PAIR),
             )
 
         def regroup_attn(m, bank):
@@ -324,6 +338,8 @@ def tile_polynomialattn_t_kernel(tc, q, k, v, out):
                 take_k(nc.vector.tensor_copy, 1, k_u, k_g_pair, k_bank)
             for n in v_halves.get(m, ()):
                 regroup_v(n)
+            if m in PART_K:
+                part_k(*PART_K[m])
             square(m, dots)
 
             if m % 2 == 1:

@@ -104,8 +104,8 @@ def tile_polynomialattn_t_kernel(tc, q, k, v, out):
         for h in range(HEADS):
             k_turned[h] = keep.tile([P, GROUPS, T], F32, name="k_turned%d" % h)
             k_parted[h] = keep.tile([P, GROUPS, PAIR, T], BF16, name="k_parted%d" % h)
-            v_codes[h] = keep.tile([P, D], U32, name="v_codes%d" % h, align_bytes=64)
-            v_scales[h] = keep.tile([P, D], U8, name="v_scales%d" % h, align_bytes=64)
+            v_codes[h] = keep.tile([P, D], U32, name="v_codes%d" % h, align_bytes=256)
+            v_scales[h] = keep.tile([P, D], U8, name="v_scales%d" % h, align_bytes=256)
 
         q_turned, x, row_sum, attn, attn_grouped, attn_codes, attn_scales = {}, {}, {}, {}, {}, {}, {}
         v_grouped, products = {}, {}
@@ -201,8 +201,8 @@ def tile_polynomialattn_t_kernel(tc, q, k, v, out):
         def quantise_attn(m):
             if not is_tile(m):
                 return
-            attn_codes[m] = hand.tile([P, P], U32, name="attn_codes", align_bytes=64)
-            attn_scales[m] = hand.tile([P, P], U8, name="attn_scales", align_bytes=64)
+            attn_codes[m] = hand.tile([P, P], U32, name="attn_codes", align_bytes=256)
+            attn_scales[m] = hand.tile([P, P], U8, name="attn_scales", align_bytes=256)
             nc.vector.quantize_mx(
                 out=attn_codes[m][:].bitcast(FP8X4),
                 scales=attn_scales[m][:],

from contextlib import ExitStack

import concourse.masks as masks
import concourse.mybir as mybir

BF16 = mybir.dt.bfloat16
F32 = mybir.dt.float32
U32 = mybir.dt.uint32
U8 = mybir.dt.uint8
FP8X4 = mybir.dt.float8_e4m3fn_x4
SQUARE = mybir.ActivationFunctionType.Square
ADD, MAX = mybir.AluOpType.add, mybir.AluOpType.max

P = 128
HEADS, S, T, D = 2, 2048, 512, 1024
EPS = 1e-4
PACK = 4
PAIR = 2
GROUPS = D // (PAIR * P)
BANK = 512
HALVES = D // BANK
TILES_PER_HEAD = S // P
TILES = HEADS * TILES_PER_HEAD
MATMULS = GROUPS * PAIR

Q_LEAD = 2
FLIP_LAG = 2
QUANT_LAG = 3
MX_LAG = 3
OUT_LAG = 5
K_STRIDE = 2
FLIPS_PER_MATMUL = 2
ATTN_FIRST, Q_FIRST, K_FIRST = 4, 1, 6
PART_K = {4: (0, 0), 5: (0, 1), 6: (0, 2), 7: (0, 3), 13: (1, 0), 15: (1, 1), 16: (1, 2), 17: (1, 3)}
PARTED_FROM = (8, 18)
WARM_MATMULS = 16
WARM_BEHIND = 3

FLOPS = 2 * 2 * HEADS * S * T * D

assert T == PACK * P and K_STRIDE % 2 == 0


def tile_polynomialattn_t_kernel(tc, q, k, v, out):
    nc = tc.nc

    q_pairs = q.rearrange("b h (r p u) d -> (b h r) p u d", p=P, u=PAIR)
    out_pairs = out.rearrange("b h (r p u) d -> (b h r) p u d", p=P, u=PAIR)
    k_pieces = k.rearrange("b h (p j) d -> (b h) j p d", j=PACK)
    v_heads = v.rearrange("b h (p j) d -> (b h) p j d", j=PACK)

    with ExitStack() as ctx:
        keep = ctx.enter_context(tc.tile_pool(name="keep", bufs=1))
        hand = ctx.enter_context(tc.tile_pool(name="hand", bufs=4))
        results = ctx.enter_context(tc.tile_pool(name="results", bufs=8))
        v_stage = ctx.enter_context(tc.tile_pool(name="v_stage", bufs=2))
        dots_banks = ctx.enter_context(tc.psum_pool(name="dots_banks", bufs=2))
        flip_banks = ctx.enter_context(tc.psum_pool(name="flip_banks", bufs=2))
        prod_banks = ctx.enter_context(tc.psum_pool(name="prod_banks", bufs=PAIR * HALVES))
        ctx.enter_context(tc.manual_schedule())

        identity = keep.tile([P, P], BF16, name="identity")
        masks.make_identity(nc, identity[:])
        identity_words = keep.tile([P, P], F32, name="identity_words")
        masks.make_identity(nc, identity_words[:])

        def keep_warm(count):
            warm = dots_banks.tile([P, T], F32, name="dots")
            for n in range(count):
                nc.tensor.matmul(out=warm[:, :P], lhsT=identity[:], rhs=identity[:], start=True, stop=True)

        keep_warm(WARM_MATMULS)

        q_raw, k_raw, v_raw = {}, {}, {}

        def load_q(r):
            q_raw[r] = keep.tile([P, PAIR, D], BF16, name="q_raw%d" % r)
            nc.sync.dma_start(out=q_raw[r][:], in_=q_pairs[r])

        def load_k(h, j):
            k_raw[(h, j)] = keep.tile([P, D], BF16, name="k_raw%d_%d" % (h, j))
            nc.sync.dma_start(out=k_raw[(h, j)][:], in_=k_pieces[h, j])

        def load_v(h):
            v_raw[h] = keep.tile([P, PACK, D], BF16, name="v_raw%d" % h)
            nc.sync.dma_start(out=v_raw[h][:], in_=v_heads[h])

        q_raw[0] = keep.tile([P, PAIR, D], BF16, name="q_raw0")
        for u in range(PAIR):
            nc.sync.dma_start(out=q_raw[0][:, u, :], in_=q_pairs[0][:, u, :])
            for j in range(PAIR):
                load_k(0, PAIR * u + j)
        load_q(1)
        load_v(0)
        load_q(2)
        load_v(1)
        load_q(3)
        for j in range(PACK):
            load_k(1, j)
        for r in range(4, TILES // PAIR):
            load_q(r)

        k_turned, k_parted, v_codes, v_scales = {}, {}, {}, {}
        for h in range(HEADS):
            k_turned[h] = keep.tile([P, GROUPS, T], F32, name="k_turned%d" % h)
            k_parted[h] = keep.tile([P, GROUPS, PAIR, T], BF16, name="k_parted%d" % h)
            v_codes[h] = keep.tile([P, D], U32, name="v_codes%d" % h, align_bytes=256)
            v_scales[h] = keep.tile([P, D], U8, name="v_scales%d" % h, align_bytes=256)

        q_turned, x, row_sum, attn, attn_grouped, attn_codes, attn_scales = {}, {}, {}, {}, {}, {}, {}
        v_grouped, products = {}, {}

        last = TILES - 1

        def is_tile(m):
            return 0 <= m < TILES

        v_halves = {1: (0, 1), 9: (2,), 11: (3,)}

        def word_flips(bank, row_tile):
            words = row_tile.bitcast(F32)
            return [(bank[:, g, :], words[:, g * P : (g + 1) * P], identity_words) for g in range(GROUPS)]

        def k_flips(bank, head, u, g_pair):
            flips = []
            for e in range(PAIR):
                for g2 in range(PAIR):
                    g = PAIR * g_pair + g2
                    words = k_raw[(head, PAIR * u + e)][:].bitcast(F32)
                    flips.append((bank[:, g2, e, :], words[:, g * P : (g + 1) * P], identity_words))
            return flips

        def attn_flips(bank, m):
            words = attn[m][:].bitcast(F32)
            return [(bank[:, u, :], words[:, u * P : (u + 1) * P], identity_words) for u in range(PAIR)]

        def weave(behind, first, flips):
            for n, flip in enumerate(flips):
                behind[first + n // FLIPS_PER_MATMUL].append(flip)

        def issue_flips(flips):
            for target, block, one in flips:
                nc.tensor.transpose(target, block, one[:])

        def multiply_qk(m, dots, keys, behind, to=None):
            to = keys if to is None else to
            for n in range(MATMULS):
                g, e = divmod(n, PAIR)
                head = m // TILES_PER_HEAD
                if m >= PARTED_FROM[head]:
                    k_part = k_parted[head][:, g, e, keys]
                else:
                    k_part = k_turned[head][:, g, keys].bitcast(BF16)[:, e : PAIR * (keys.stop - keys.start) : PAIR]
                nc.tensor.matmul(
                    out=dots[:, to],
                    lhsT=q_turned[m][:, g, :].bitcast(BF16)[:, e : PAIR * P : PAIR],
                    rhs=k_part,
                    start=(n == 0),
                    stop=(n == MATMULS - 1),
                )
                issue_flips(behind[n])

        def square(m, dots):
            x[m] = hand.tile([P, T], F32, name="x")
            row_sum[m] = hand.tile([P, 1], F32, name="row_sum")
            nc.scalar.activation(out=x[m][:], in_=dots[:], func=SQUARE, accum_out=row_sum[m][:])

        def normalise(m):
            if not is_tile(m):
                return
            denom = hand.tile([P, 1], F32, name="denom")
            nc.vector.tensor_scalar_max(out=denom[:], in0=row_sum[m][:], scalar1=EPS)
            inverse = hand.tile([P, 1], F32, name="inverse")
            nc.vector.reciprocal(out=inverse[:], in_=denom[:])
            attn[m] = hand.tile([P, T], BF16, name="attn")
            nc.vector.tensor_scalar_mul(out=attn[m][:], in0=x[m][:], scalar1=inverse[:])

        def take_q(copy, m, bank):
            q_turned[m] = hand.tile([P, GROUPS, P], F32, name="q_turned")
            copy(out=q_turned[m][:], in_=bank[:])

        def take_k(copy, head, u, g_pair, bank, g2=None):
            groups = slice(0, PAIR) if g2 is None else slice(g2, g2 + 1)
            copy(
                out=k_turned[head][
                    :, PAIR * g_pair + groups.start : PAIR * g_pair + groups.stop, u * PAIR * P : (u + 1) * PAIR * P
                ].rearrange("p g (n e) -> p g n e", e=PAIR),
                in_=bank[:, groups, :, :].rearrange("p g e n -> p g n e"),
            )

        def part_k(head, g):
            nc.vector.tensor_copy(
                out=k_parted[head][:, g, :, :],
                in_=k_turned[head][:, g, :].bitcast(BF16).rearrange("p (c e) -> p e c", e=PAIR),
            )

        def regroup_attn(m, bank):
            attn_grouped[m] = hand.tile([P, P, PAIR], F32, name="attn_grouped", align_bytes=64)
            nc.vector.tensor_copy(out=attn_grouped[m][:], in_=bank[:].rearrange("p u s -> p s u"))

        def quantise_attn(m):
            if not is_tile(m):
                return
            attn_codes[m] = hand.tile([P, P], U32, name="attn_codes", align_bytes=256)
            attn_scales[m] = hand.tile([P, P], U8, name="attn_scales", align_bytes=256)
            nc.vector.quantize_mx(
                out=attn_codes[m][:].bitcast(FP8X4),
                scales=attn_scales[m][:],
                in_=attn_grouped[m][:].rearrange("p s u -> p (s u)").bitcast(BF16),
            )

        def regroup_v(n):
            cols = slice((n % HALVES) * BANK, (n % HALVES + 1) * BANK)
            v_grouped[n] = v_stage.tile([P, BANK, PACK], BF16, name="v_grouped", align_bytes=64)
            nc.vector.tensor_copy(
                out=v_grouped[n][:], in_=v_raw[n // HALVES][:, :, cols].rearrange("p j d -> p d j")
            )

        def quantise_v(n):
            cols = slice((n % HALVES) * BANK, (n % HALVES + 1) * BANK)
            nc.vector.quantize_mx(
                out=v_codes[n // HALVES][:, cols].bitcast(FP8X4),
                scales=v_scales[n // HALVES][:, cols],
                in_=v_grouped[n][:].rearrange("p d j -> p (d j)"),
            )

        def multiply_mx(m, banks=prod_banks, tag="product", pieces=range(HALVES), width=BANK):
            if not is_tile(m):
                return
            h = m // TILES_PER_HEAD
            for piece in pieces:
                cols = slice(piece * width, (piece + 1) * width)
                products[(m, piece)] = banks.tile([P, BANK], F32, name="product", tag=tag)
                nc.tensor.matmul_mx(
                    out=products[(m, piece)][:, :width],
                    lhsT=attn_codes[m][:].bitcast(FP8X4),
                    lhsT_scale=attn_scales[m][:],
                    rhs=v_codes[h][:, cols].bitcast(FP8X4),
                    rhs_scale=v_scales[h][:, cols],
                    start=True,
                    stop=True,
                )

        def store_products(m):
            if not is_tile(m):
                return
            result = results.tile([P, D], F32, name="result")
            nc.scalar.copy(out=result[:, :BANK], in_=products[(m, 0)][:])
            nc.vector.tensor_copy(out=result[:, BANK:], in_=products[(m, 1)][:])
            nc.sync.dma_start(out=out_pairs[m // PAIR][:, m % PAIR, :], in_=result[:])

        def store_piece(m, copy, piece, width=BANK):
            result = results.tile([P, width], F32, name="result_piece%d" % width)
            copy(out=result[:], in_=products[(m, piece)][:, :width])
            nc.sync.dma_start(out=out_pairs[m // PAIR][:, m % PAIR, piece * width : (piece + 1) * width], in_=result[:])

        def q_words(m):
            return q_raw[m // PAIR][:, m % PAIR, :]

        def no_flips():
            return [[] for n in range(MATMULS)]

        first_k = [prod_banks.tile([P, PAIR, PAIR, P], F32, name="k_bank", tag="product") for part in range(PACK)]
        k_parts = [k_flips(first_k[part], 0, *divmod(part, PAIR)) for part in range(PACK)]
        def flip_piece(piece):
            u, e = divmod(piece, PAIR)
            for part in (PAIR * u, PAIR * u + 1):
                issue_flips(k_parts[part][PAIR * e : PAIR * (e + 1)])

        def flip_q(m):
            bank = flip_banks.tile([P, GROUPS, P], F32, name="q_bank", tag="flip_bank")
            return bank, word_flips(bank, q_words(m))

        def start_q(copy, m):
            q_bank, flips = flip_q(m)
            issue_flips(flips)
            keep_warm(WARM_BEHIND)
            take_q(copy, m, q_bank)

        start_q(nc.scalar.copy, 0)
        for piece in range(PAIR):
            flip_piece(piece)
            keep_warm(WARM_BEHIND)
        for g2 in range(PAIR):
            take_k(nc.scalar.copy, 0, 0, 0, first_k[0], g2)
            take_k(nc.vector.tensor_copy, 0, 0, 1, first_k[1], g2)
        start_q(nc.vector.tensor_copy, 1)

        first_dots = [dots_banks.tile([P, T], F32, name="dots") for m in range(PAIR)]
        behind = no_flips()
        for part in (PAIR, PAIR + 1):
            weave(behind, 1 + 3 * (part - PAIR), k_parts[part][:PAIR])
            weave(behind, 3 + 3 * (part - PAIR), k_parts[part][PAIR:])
        multiply_qk(0, first_dots[0], slice(0, T // 2), behind)
        take_k(nc.vector.tensor_copy, 0, 1, 0, first_k[2])
        take_k(nc.scalar.copy, 0, 1, 1, first_k[3])
        multiply_qk(1, first_dots[1], slice(0, T // 2), no_flips())
        for m in range(PAIR):
            behind = no_flips()
            q_bank, flips = flip_q(m + Q_LEAD)
            weave(behind, Q_FIRST, flips)
            multiply_qk(m, first_dots[m], slice(T // 2, T), behind)
            take_q(nc.scalar.copy, m + Q_LEAD, q_bank)
            square(m, first_dots[m])
        regroup_v(v_halves[1][0])
        normalise(0)
        regroup_v(v_halves[1][1])

        for m in range(PAIR, last):
            quantise_attn(m - QUANT_LAG)
            store_products(m - OUT_LAG)

            behind = no_flips()
            attn_bank, k_bank, q_bank = None, None, None
            if is_tile(m - FLIP_LAG):
                attn_bank = flip_banks.tile([P, PAIR, P], F32, name="attn_bank", tag="flip_bank")
                weave(behind, ATTN_FIRST, attn_flips(attn_bank, m - FLIP_LAG))
            if is_tile(m + Q_LEAD):
                q_bank, flips = flip_q(m + Q_LEAD)
                weave(behind, Q_FIRST, flips)
            part, odd = divmod(m - TILES_PER_HEAD + K_STRIDE * PACK, K_STRIDE)
            k_u, k_g_pair = divmod(part, PAIR)
            if 0 <= part < PACK and odd == 0:
                k_bank = flip_banks.tile([P, PAIR, PAIR, P], F32, name="k_bank", tag="flip_bank")
                weave(behind, K_FIRST, k_flips(k_bank, 1, k_u, k_g_pair))

            dots = dots_banks.tile([P, T], F32, name="dots")
            multiply_qk(m, dots, slice(0, T), behind)

            normalise(m - 1)
            if attn_bank is not None:
                regroup_attn(m - FLIP_LAG, attn_bank)
            if q_bank is not None:
                take_q(nc.scalar.copy, m + Q_LEAD, q_bank)
            for n in v_halves.get(m - 1, ()):
                quantise_v(n)
            if k_bank is not None:
                take_k(nc.vector.tensor_copy, 1, k_u, k_g_pair, k_bank)
            for n in v_halves.get(m, ()):
                regroup_v(n)
            if m in PART_K:
                part_k(*PART_K[m])
            square(m, dots)

            if m % 2 == 1:
                multiply_mx(m - MX_LAG - 1)
                multiply_mx(m - MX_LAG)

        quantise_attn(last - QUANT_LAG)
        store_products(last - OUT_LAG)
        x[last] = hand.tile([P, T], F32, name="x")
        half_sums = hand.tile([P, PAIR], F32, name="half_sums")

        def multiply_half(half, attn_tile):
            bank = flip_banks.tile([P, PAIR, P], F32, name="attn_bank", tag="flip_bank")
            behind = no_flips()
            weave(behind, 2, attn_flips(bank, attn_tile))
            dots = dots_banks.tile([P, T], F32, name="dots")
            multiply_qk(last, dots, slice(half * T // 2, (half + 1) * T // 2), behind, to=slice(0, T // 2))
            return dots, bank

        def square_half(half, dots):
            nc.scalar.activation(
                out=x[last][:, half * T // 2 : (half + 1) * T // 2],
                in_=dots[:, : T // 2],
                func=SQUARE,
                accum_out=half_sums[:, half : half + 1],
            )

        dots, bank = multiply_half(0, last - 2)
        square_half(0, dots)
        multiply_mx(last - 4)
        multiply_mx(last - 3)
        normalise(last - 1)
        regroup_attn(last - 2, bank)
        store_piece(last - 4, nc.scalar.copy, 0)
        store_piece(last - 4, nc.vector.tensor_copy, 1)
        quantise_attn(last - 2)
        store_piece(last - 3, nc.scalar.copy, 0)
        store_piece(last - 3, nc.vector.tensor_copy, 1)
        dots, bank = multiply_half(1, last - 1)
        square_half(1, dots)
        regroup_attn(last - 1, bank)
        quantise_attn(last - 1)
        multiply_mx(last - 2)
        multiply_mx(last - 1)

        denom = hand.tile([P, 1], F32, name="denom")
        nc.vector.tensor_scalar(
            out=denom[:], in0=half_sums[:, 0:1], scalar1=half_sums[:, 1:2], scalar2=EPS, op0=ADD, op1=MAX
        )
        inverse = hand.tile([P, 1], F32, name="inverse")
        nc.vector.reciprocal(out=inverse[:], in_=denom[:])
        attn[last] = hand.tile([P, T], BF16, name="attn")
        bank = flip_banks.tile([P, PAIR, P], F32, name="attn_bank", tag="flip_bank")
        for half, flip in enumerate(attn_flips(bank, last)):
            keys = slice(half * T // 2, (half + 1) * T // 2)
            nc.vector.tensor_scalar_mul(out=attn[last][:, keys], in0=x[last][:, keys], scalar1=inverse[:])
            issue_flips([flip])
        store_piece(last - 2, nc.scalar.copy, 0)
        store_piece(last - 2, nc.vector.tensor_copy, 1)
        regroup_attn(last, bank)
        quantise_attn(last)
        store_piece(last - 1, nc.scalar.copy, 0)
        store_piece(last - 1, nc.scalar.copy, 1)
        quarter = BANK // 2
        multiply_mx(last, dots_banks, "dots", range(0, 2), quarter)
        multiply_mx(last, prod_banks, "product", range(2, 4), quarter)
        for piece in range(4):
            store_piece(last, nc.vector.tensor_copy if piece % 2 else nc.scalar.copy, piece, quarter)
